import numpy as np
import ml_dtypes


def mxq(x, axis, fmt="e4m3"):
    dtype, down = {"e4m3": (ml_dtypes.float8_e4m3fn, 7), "e5m2": (ml_dtypes.float8_e5m2, 14)}[fmt]
    v = np.moveaxis(np.asarray(x, np.float32).astype(ml_dtypes.bfloat16).astype(np.float64), axis, -1)
    blocks = v.reshape(v.shape[:-1] + (-1, 32))
    amax = np.abs(blocks).max(-1, keepdims=True)
    byte = np.maximum(np.where(amax > 0, np.frexp(amax)[1] - 1 + 127, 0) - down, 1)
    scale = np.exp2(byte - 127.0)
    codes = (blocks / scale).astype(np.float32).astype(dtype).astype(np.float64)
    return np.moveaxis((codes * scale).reshape(v.shape), -1, axis)


WIDE = False


def mx_kscale(k):
    if not WIDE:
        return np.ones(k)
    levels = np.array([10, -10, 5, -5, 0])
    a = np.random.permutation(np.resize(levels, k // 512 * 4)).reshape(k // 512, 4)
    idx = np.arange(k)
    return np.exp2(a[idx // 512, idx % 128 // 32])


BF16 = ml_dtypes.bfloat16


def bf(x):
    return np.asarray(x, np.float32).astype(BF16)


def f64(x):
    return np.asarray(x).astype(np.float64)


B, P, D, NL, T, E, G = 2, 128, 16384, 8, 2, 1, 2
WW = NL * NL * T
WG = WW * G
CLIP = 1.0
LOG_2PI = np.log(2.0 * np.pi)


def clip(v):
    return np.clip(v, -CLIP, CLIP)


def gaussian_scale(m1, v1, m2, v2):
    add = np.exp(2.0 * v1) + np.exp(2.0 * v2)
    return (-0.5 * (LOG_2PI + np.log(add) + (m1 - m2) ** 2 / add)).sum(-1)


def setup_inputs():
    s = mx_kscale(D)
    return {"x_next": bf(np.random.standard_normal((B, P, D)) * s),
            "cs_scale": bf(np.random.standard_normal((B, P, NL, NL, T, E)) * 1.2 - 3.4),
            "cs_mu": bf(clip(np.random.standard_normal((B, P, NL, NL, T, E, G)) * 0.55)),
            "cs_var": bf(np.random.standard_normal((B, P, NL, NL, T, E, G)) * 0.5 - 0.5),
            "mask_here": bf(0.5 + np.random.random((B, P))),
            "mask_next": bf(0.5 + np.random.random((B, P))),
            "tw_w": bf(np.random.standard_normal((D, WW)) / np.sqrt(D) / s[:, None]),
            "tw_b": bf(np.random.standard_normal(WW) * 0.3),
            "tpm_w": bf(np.random.standard_normal((D, WG)) / np.sqrt(D) / s[:, None]),
            "tpm_b": bf(np.random.standard_normal(WG) * 0.3),
            "tpv_w": bf(np.random.standard_normal((D, WG)) / np.sqrt(D) / s[:, None]),
            "tpv_b": bf(np.random.standard_normal(WG) * 0.3)}


def reference(x_next, cs_scale, cs_mu, cs_var, mask_here, mask_next, tw_w, tw_b, tpm_w, tpm_b, tpv_w, tpv_b):
    xq = mxq(f64(x_next).reshape(B * P, D), 1, "e4m3")
    t_weight = ((xq @ mxq(f64(tw_w), 0, "e4m3")) + f64(tw_b)).reshape(B, P, NL, NL, T)[:, :, None, :, :, None, None, :]
    t_p_mu = clip(((xq @ mxq(f64(tpm_w), 0, "e4m3")) + f64(tpm_b)).reshape(B, P, NL, NL, T, G))[:, :, None, :, :, None, None, :, :]
    t_p_var = clip(((xq @ mxq(f64(tpv_w), 0, "e4m3")) + f64(tpv_b)).reshape(B, P, NL, NL, T, G))[:, :, None, :, :, None, None, :, :]
    a_mu = f64(cs_mu)[:, :, :, :, None, :, :, None, :]
    a_var = f64(cs_var)[:, :, :, :, None, :, :, None, :]
    m_next = f64(mask_next)[:, :, None, None, None, None, None, None]
    m_here = f64(mask_here)[:, :, None, None, None, None, None, None]
    csp_scale = gaussian_scale(a_mu, a_var, t_p_mu, t_p_var)
    csp_scale = csp_scale * m_next + f64(cs_scale)[:, :, :, :, None, :, :, None] + t_weight * m_next
    return csp_scale * m_here

@@ -1,0 +1,325 @@
+import math
+from contextlib import ExitStack
+
+import concourse.mybir as mybir
+from concourse.masks import make_identity
+
+FP8X4 = mybir.dt.float8_e4m3fn_x4
+BF16 = mybir.dt.bfloat16
+F32 = mybir.dt.float32
+U32 = mybir.dt.uint32
+U8 = mybir.dt.uint8
+ALU = mybir.AluOpType
+ACT = mybir.ActivationFunctionType
+
+P = 128
+B = 2
+K = 16384
+NL, T, G = 8, 2, 2
+KU = NL * T
+PLANE = NL * NL * KU
+W_WEIGHT = NL * NL * T
+W_GAUSS = W_WEIGHT * G
+CLIP = 1.0
+LOG_2PI = math.log(2.0 * math.pi)
+
+PACK = 4
+K_PASS = P * PACK
+CHUNK = 4096
+X_PASSES = CHUNK // (PACK * B * P)
+X_CHUNKS = K // (X_PASSES * K_PASS)
+
+FLOPS = 2 * B * P * K * (W_WEIGHT + 2 * W_GAUSS)
+
+
+def tile_chainlveg_pb_k_kernel(
+    tc, x_next, cs_scale, cs_mu, cs_var, mask_here, mask_next, tw_w, tw_b, tpm_w, tpm_b, tpv_w, tpv_b, out
+):
+    nc = tc.nc
+    with ExitStack() as stack:
+        const = stack.enter_context(tc.tile_pool(name="const", bufs=1))
+        w_in = stack.enter_context(tc.tile_pool(name="w_in", bufs=4))
+        w_mx = stack.enter_context(tc.tile_pool(name="w_mx", bufs=2))
+        big = stack.enter_context(tc.tile_pool(name="big", bufs=4))
+        psum_t = stack.enter_context(tc.psum_pool(name="psum_t", bufs=4))
+        psum_acc = stack.enter_context(tc.psum_pool(name="psum_acc", bufs=2))
+        stack.enter_context(tc.manual_schedule())
+
+        ident_f = const.tile([P, P], F32, name="ident_f")
+        make_identity(nc, ident_f)
+        ident_b = const.tile([P, P], BF16, name="ident_b")
+        make_identity(nc, ident_b)
+
+        mean1 = const.tile([P, B, W_GAUSS], BF16, name="mean1")
+        nc.scalar.dma_start(out=mean1, in_=cs_mu.rearrange("b p i j t e g -> p b (i j t e g)"))
+        log_std1 = const.tile([P, B, W_GAUSS], BF16, name="log_std1")
+        nc.scalar.dma_start(out=log_std1, in_=cs_var.rearrange("b p i j t e g -> p b (i j t e g)"))
+        weight1 = const.tile([P, B, W_WEIGHT], BF16, name="weight1")
+        nc.scalar.dma_start(out=weight1, in_=cs_scale.rearrange("b p i j t e -> p b (i j t e)"))
+
+        mask_rows = const.tile([P, P], BF16, name="mask_rows")
+        nc.vector.memset(mask_rows, 0.0)
+        nc.scalar.dma_start(out=mask_rows[0:B, :], in_=mask_here)
+        nc.scalar.dma_start(out=mask_rows[B : 2 * B, :], in_=mask_next)
+        mask_cols = psum_t.tile([P, P], BF16, name="mask_cols", tag="xt")
+        nc.tensor.transpose(out=mask_cols, in_=mask_rows, identity=ident_b)
+        factors = const.tile([P, 2 * B], F32, name="factors")
+        nc.vector.tensor_copy(out=factors, in_=mask_cols[:, 0 : 2 * B])
+        both = const.tile([P, B], F32, name="both")
+        nc.vector.tensor_tensor(out=both, in0=factors[:, 0:B], in1=factors[:, B : 2 * B], op=ALU.mult)
+        minus_half = const.tile([P, B], F32, name="minus_half")
+        nc.vector.tensor_scalar(out=minus_half, in0=both, scalar1=-0.5, scalar2=None, op0=ALU.mult)
+
+        var1 = const.tile([P, B, W_GAUSS], F32, name="var1")
+        nc.scalar.activation(out=var1, in_=log_std1, func=ACT.Exp, scale=2.0)
+        weight1_here = const.tile([P, B, W_WEIGHT], F32, name="weight1_here")
+        for b in range(B):
+            nc.vector.tensor_scalar(
+                out=weight1_here[:, b], in0=weight1[:, b], scalar1=factors[:, b : b + 1], scalar2=None, op0=ALU.mult
+            )
+
+        bias = {}
+
+        def load_biases():
+            for key, vector, width in (("var", tpv_b, W_GAUSS), ("mean", tpm_b, W_GAUSS), ("weight", tw_b, W_WEIGHT)):
+                bias[key] = const.tile([P, width], BF16, name="bias_" + key)
+                nc.sync.dma_start(out=bias[key], in_=vector.partition_broadcast(P))
+
+        x_codes = const.tile([P, K // K_PASS * B * P], U32, name="x_codes", align_bytes=64)
+        x_scales = const.tile([P, K // K_PASS * B * P], U8, name="x_scales", align_bytes=64)
+
+        def transpose_x(n):
+            cols = X_PASSES * K_PASS
+            x_raw = big.tile([P, B * cols], BF16, name="x_raw", tag="half", align_bytes=64)
+            nc.sync.dma_start(
+                out=x_raw.rearrange("r (b k) -> r b k", b=B),
+                in_=x_next[:, :, n * cols : (n + 1) * cols].rearrange("b r k -> r b k"),
+            )
+            words = x_raw.bitcast(F32).rearrange("r (b c p u) -> r b c u p", b=B, c=X_PASSES, u=2)
+            x_grouped = big.tile([P, CHUNK], BF16, name="x_grouped", tag="full", align_bytes=64)
+            grouped_words = x_grouped.bitcast(F32).rearrange("p (c b r u) -> p c b r u", c=X_PASSES, b=B, u=2)
+            for c in range(X_PASSES):
+                xt = psum_t.tile([P, B, 2, P], F32, name="xt", tag="xt")
+                for b in range(B):
+                    for u in range(2):
+                        nc.tensor.transpose(out=xt[:, b, u, :], in_=words[:, b, c, u, :], identity=ident_f)
+                nc.scalar.copy(out=grouped_words[:, c], in_=xt.rearrange("p b u r -> p b r u"))
+            return x_grouped
+
+        def quantise_x(n, x_grouped):
+            cols = slice(n * CHUNK // PACK, (n + 1) * CHUNK // PACK)
+            nc.vector.quantize_mx(out=x_codes[:, cols].bitcast(FP8X4), scales=x_scales[:, cols], in_=x_grouped)
+
+        def regroup_weights(w, width, s, vector_passes):
+            passes = CHUNK // (PACK * width)
+            w_raw = w_in.tile([P, CHUNK], BF16, name="w_raw")
+            rows = w[s * passes * K_PASS : (s + 1) * passes * K_PASS, :]
+            nc.sync.dma_start(
+                out=w_raw.rearrange("p (c e) -> p c e", c=passes),
+                in_=rows.rearrange("(c p j) w -> p c (j w)", c=passes, j=PACK),
+            )
+            w_grouped = w_mx.tile([P, CHUNK], BF16, name="w_grouped", align_bytes=64)
+            src = w_raw.rearrange("p (c j v i) -> p c v j i", c=passes, j=PACK, i=4)
+            dst = w_grouped.rearrange("p (c v i j) -> p c v j i", c=passes, i=4, j=PACK)
+            for c in range(passes):
+                if c < vector_passes:
+                    nc.vector.tensor_copy(out=dst[:, c], in_=src[:, c])
+                else:
+                    nc.scalar.copy(out=dst[:, c], in_=src[:, c])
+            return w_grouped
+
+        def quantise_and_multiply(w_grouped, width, s, acc):
+            passes = CHUNK // (PACK * width)
+            w_codes = w_mx.tile([P, CHUNK // PACK], U32, name="w_codes", align_bytes=64)
+            w_scales = w_mx.tile([P, CHUNK // PACK], U8, name="w_scales", align_bytes=64)
+            nc.vector.quantize_mx(out=w_codes.bitcast(FP8X4), scales=w_scales, in_=w_grouped)
+            for c in range(passes):
+                k_pass = s * passes + c
+                w_cols = slice(c * width, (c + 1) * width)
+                for b in range(B):
+                    x_cols = slice((k_pass * B + b) * P, (k_pass * B + b + 1) * P)
+                    nc.tensor.matmul_mx(
+                        out=acc[b],
+                        lhsT=x_codes[:, x_cols].bitcast(FP8X4),
+                        lhsT_scale=x_scales[:, x_cols],
+                        rhs=w_codes[:, w_cols].bitcast(FP8X4),
+                        rhs_scale=w_scales[:, w_cols],
+                        start=(k_pass == 0),
+                        stop=(k_pass == K // K_PASS - 1),
+                    )
+
+        def plane_views(child, parent, g, t):
+            c = child.rearrange("p (i j t g) -> p t g i j", i=NL, j=NL, t=T, g=G)[:, t, g]
+            q = parent.rearrange("p (j c g) -> p g j c", j=NL, c=KU, g=G)[:, g]
+            shape = [P, NL, NL, KU]
+            return c.unsqueeze(3).to_broadcast(shape), q.unsqueeze(1).to_broadcast(shape)
+
+        def as_plane(ap):
+            return ap.rearrange("p (i j c) -> p i j c", i=NL, j=NL)
+
+        def flat(ap):
+            return ap.rearrange("p t n -> p (t n)")
+
+        def parent_term(acc, key):
+            term = const.tile([P, B, W_GAUSS], F32, name="parent_" + key)
+            for b in range(B):
+                nc.vector.tensor_tensor(out=term[:, b], in0=acc[b], in1=bias[key], op=ALU.add)
+            nc.vector.tensor_scalar(out=term, in0=term, scalar1=CLIP, scalar2=-CLIP, op0=ALU.min, op1=ALU.max)
+            return term
+
+        log_sum, precision, square, partial, result = {}, {}, {}, {}, {}
+        parent = {}
+
+        def sum_of_variances(pair):
+            b, g = divmod(pair, G)
+            if g == 0:
+                log_sum[b] = big.tile([P, G, T, PLANE], F32, name="log_sum", tag="full", align_bytes=64)
+            for t in range(T):
+                c, q = plane_views(var1[:, b], parent["var"][:, b], g, t)
+                nc.vector.tensor_tensor(out=as_plane(log_sum[b][:, g, t]), in0=c, in1=q, op=ALU.add)
+
+        def log_of_sum(pair):
+            b, g = divmod(pair, G)
+            nc.scalar.activation(out=log_sum[b][:, g], in_=log_sum[b][:, g], func=ACT.Ln)
+
+        def one_over_sum(pair):
+            b, g = divmod(pair, G)
+            if g == 0:
+                precision[b] = big.tile([P, G, T, PLANE], F32, name="precision", tag="full", align_bytes=64)
+            nc.scalar.activation(out=precision[b][:, g], in_=log_sum[b][:, g], func=ACT.Exp, scale=-1.0)
+
+        def log_terms(pair):
+            b, g = divmod(pair, G)
+            if g == 0:
+                partial[b] = big.tile([P, T, PLANE], F32, name="partial", tag="half", align_bytes=64)
+            for t in range(T):
+                so_far = partial[b][:, t].rearrange("p (n c) -> p n c", c=KU)
+                if g == 0:
+                    before = weight1_here[:, b].rearrange("p (n t) -> p t n", t=T)[:, t]
+                    before = before.unsqueeze(2).to_broadcast([P, NL * NL, KU])
+                else:
+                    before = so_far
+                nc.vector.scalar_tensor_tensor(
+                    out=so_far,
+                    in0=log_sum[b][:, g, t].rearrange("p (n c) -> p n c", c=KU),
+                    scalar=minus_half[:, b : b + 1],
+                    in1=before,
+                    op0=ALU.mult,
+                    op1=ALU.add,
+                )
+
+        def difference(pair):
+            b, g = divmod(pair, G)
+            if g == 0:
+                square[b] = big.tile([P, G, T, PLANE], F32, name="square", tag="full", align_bytes=64)
+            for t in range(T):
+                c, q = plane_views(mean1[:, b], parent["mean"][:, b], g, t)
+                nc.vector.tensor_tensor(out=as_plane(square[b][:, g, t]), in0=c, in1=q, op=ALU.subtract)
+
+        def square_difference(pair):
+            b, g = divmod(pair, G)
+            nc.scalar.activation(out=square[b][:, g], in_=square[b][:, g], func=ACT.Square)
+
+        def weigh(pair):
+            b, g = divmod(pair, G)
+            nc.vector.scalar_tensor_tensor(
+                out=flat(square[b][:, g]),
+                in0=flat(square[b][:, g]),
+                scalar=minus_half[:, b : b + 1],
+                in1=flat(precision[b][:, g]),
+                op0=ALU.mult,
+                op1=ALU.mult,
+            )
+
+        def sum_up(b):
+            nc.vector.tensor_tensor(
+                out=flat(square[b][:, 0]), in0=flat(square[b][:, 0]), in1=flat(square[b][:, 1]), op=ALU.add
+            )
+            result[b] = big.tile([P, T * PLANE], F32, name="result", tag="half", align_bytes=64)
+            nc.vector.tensor_tensor(
+                out=result[b].rearrange("p (n t u) -> p n t u", t=T, u=T),
+                in0=square[b][:, 0].rearrange("p t (n u) -> p n t u", u=T),
+                in1=partial[b].rearrange("p t (n u) -> p n t u", u=T),
+                op=ALU.add,
+            )
+
+        def add_transition_weight(b, acc):
+            tw = const.tile([P, W_WEIGHT], F32, name="tw%d" % b)
+            nc.vector.tensor_tensor(out=tw, in0=acc[b], in1=bias["weight"], op=ALU.add)
+            tw_t = const.tile([P, NL * NL, T, T], F32, name="tw_t%d" % b)
+            nc.vector.tensor_scalar(
+                out=tw_t,
+                in0=tw.rearrange("p (n u) -> p n u", u=T).unsqueeze(2).to_broadcast([P, NL * NL, T, T]),
+                scalar1=-LOG_2PI,
+                scalar2=both[:, b : b + 1],
+                op0=ALU.add,
+                op1=ALU.mult,
+            )
+            rows = result[b].rearrange("p (i m) -> p i m", i=NL)
+            nc.vector.tensor_tensor(
+                out=rows,
+                in0=rows,
+                in1=tw_t.rearrange("p n t u -> p (n t u)").unsqueeze(1).to_broadcast([P, NL, NL * NL * T * T]),
+                op=ALU.add,
+            )
+            nc.sync.dma_start(out=out[b].rearrange("p i j k t e u -> p (i j k t e u)"), in_=result[b])
+
+        streams = (
+            ("var", tpv_w, W_GAUSS, 3),
+            ("mean", tpm_w, W_GAUSS, 2),
+            ("weight", tw_w, W_WEIGHT, 0),
+        )
+        pieces = []
+        for key, w, width, vector_passes in streams:
+            for s in range(K * width // (P * CHUNK)):
+                pieces.append((key, w, width, vector_passes, s))
+        var_done = K * W_GAUSS // (P * CHUNK)
+        mean_done = 2 * var_done
+        pairs = B * G
+
+        acc = {}
+        grouped = {}
+        x_grouped = {}
+        for n in range(len(pieces) + 1):
+            v = n - var_done - 1
+            m = n - mean_done - 1
+            if 0 <= v < pairs:
+                log_of_sum(v)
+            if pairs <= v < 2 * pairs:
+                one_over_sum(v - pairs)
+            if 0 <= m < pairs:
+                square_difference(m)
+            if n < X_CHUNKS:
+                x_grouped[n] = transpose_x(n)
+            if n < len(pieces):
+                key, w, width, vector_passes, s = pieces[n]
+                grouped[n] = regroup_weights(w, width, s, vector_passes)
+            if n == X_CHUNKS - 1:
+                load_biases()
+            if 1 <= n <= X_CHUNKS:
+                quantise_x(n - 1, x_grouped[n - 1])
+            if n >= 1:
+                key, w, width, vector_passes, s = pieces[n - 1]
+                if s == 0:
+                    acc[key] = [psum_acc.tile([P, width], F32, name="acc", tag="acc%d" % b) for b in range(B)]
+                quantise_and_multiply(grouped[n - 1], width, s, acc[key])
+            if n == var_done:
+                parent["log_std"] = parent_term(acc["var"], "var")
+                parent["var"] = const.tile([P, B, W_GAUSS], F32, name="var2")
+                nc.scalar.activation(out=parent["var"], in_=parent["log_std"], func=ACT.Exp, scale=2.0)
+                sum_of_variances(0)
+            if 0 <= v < pairs - 1:
+                sum_of_variances(v + 1)
+            if pairs <= v < 2 * pairs:
+                log_terms(v - pairs)
+            if n == mean_done:
+                parent["mean"] = parent_term(acc["mean"], "mean")
+                difference(0)
+            if 0 <= m < pairs - 1:
+                difference(m + 1)
+            if 0 <= m < pairs:
+                weigh(m)
+                if m % G == G - 1:
+                    sum_up(m // G)
+        for b in range(B):
+            add_transition_weight(b, acc["weight"])

@@ -43,7 +43,6 @@ def tile_chainlveg_pb_k_kernel(
         big = stack.enter_context(tc.tile_pool(name="big", bufs=4))
         psum_t = stack.enter_context(tc.psum_pool(name="psum_t", bufs=4))
         psum_acc = stack.enter_context(tc.psum_pool(name="psum_acc", bufs=2))
-        stack.enter_context(tc.manual_schedule())
 
         ident_f = const.tile([P, P], F32, name="ident_f")
         make_identity(nc, ident_f)

@@ -23,6 +23,13 @@ W_GAUSS = W_WEIGHT * G
 CLIP = 1.0
 LOG_2PI = math.log(2.0 * math.pi)
 
+JG = 2
+JGROUPS = NL // JG
+PART = NL * JG * T
+GROUPS = G * JGROUPS
+HALVES = 2
+GCOLS = NL * JG * NL * T * T
+
 PACK = 4
 K_PASS = P * PACK
 CHUNK = 4096
@@ -38,9 +45,10 @@ def tile_chainlveg_pb_k_kernel(
     nc = tc.nc
     with ExitStack() as stack:
         const = stack.enter_context(tc.tile_pool(name="const", bufs=1))
-        w_in = stack.enter_context(tc.tile_pool(name="w_in", bufs=4))
-        w_mx = stack.enter_context(tc.tile_pool(name="w_mx", bufs=2))
-        big = stack.enter_context(tc.tile_pool(name="big", bufs=4))
+        raw = stack.enter_context(tc.tile_pool(name="raw", bufs=8))
+        regrouped = stack.enter_context(tc.tile_pool(name="regrouped", bufs=5))
+        w_mx = stack.enter_context(tc.tile_pool(name="w_mx", bufs=3))
+        roots = stack.enter_context(tc.tile_pool(name="roots", bufs=2))
         psum_t = stack.enter_context(tc.psum_pool(name="psum_t", bufs=4))
         psum_acc = stack.enter_context(tc.psum_pool(name="psum_acc", bufs=2))
 
@@ -69,13 +77,75 @@ def tile_chainlveg_pb_k_kernel(
         minus_half = const.tile([P, B], F32, name="minus_half")
         nc.vector.tensor_scalar(out=minus_half, in0=both, scalar1=-0.5, scalar2=None, op0=ALU.mult)
 
-        var1 = const.tile([P, B, W_GAUSS], F32, name="var1")
-        nc.scalar.activation(out=var1, in_=log_std1, func=ACT.Exp, scale=2.0)
-        weight1_here = const.tile([P, B, W_WEIGHT], F32, name="weight1_here")
-        for b in range(B):
-            nc.vector.tensor_scalar(
-                out=weight1_here[:, b], in0=weight1[:, b], scalar1=factors[:, b : b + 1], scalar2=None, op0=ALU.mult
-            )
+        weight1_here = const.tile([P, B, NL * NL, T, T], F32, name="weight1_here")
+
+        def child_weights():
+            for b in range(B):
+                nc.vector.tensor_scalar(
+                    out=weight1_here[:, b],
+                    in0=weight1[:, b]
+                    .rearrange("p (n t) -> p n t", t=T)
+                    .unsqueeze(3)
+                    .to_broadcast([P, NL * NL, T, T]),
+                    scalar1=factors[:, b : b + 1],
+                    scalar2=None,
+                    op0=ALU.mult,
+                )
+
+        ones_c = const.tile([P, PART], BF16, name="ones_c")
+        nc.vector.tensor_tensor(out=ones_c, in0=ident_b[:, 0:PART], in1=ident_b[:, PART : 2 * PART], op=ALU.add)
+        ones_q = const.tile([P, PART], BF16, name="ones_q")
+        nc.vector.tensor_tensor(
+            out=ones_q, in0=ident_b[:, 2 * PART : 3 * PART], in1=ident_b[:, 3 * PART : 4 * PART], op=ALU.add
+        )
+        spread = {}
+        for key, sign in (("var", 1.0), ("mean", -1.0)):
+            spread[key] = const.tile([P, GCOLS], BF16, name="spread_" + key)
+            for t in range(T):
+                nc.vector.tensor_copy(
+                    out=spread[key].rearrange("p (a k t u) -> p t a k u", a=NL * JG, k=NL, t=T)[:, t],
+                    in_=ones_c.rearrange("p (a t) -> p t a", t=T)[:, t]
+                    .unsqueeze(2)
+                    .unsqueeze(3)
+                    .to_broadcast([P, NL * JG, NL, T]),
+                )
+            for t in range(T):
+                cols_t = spread[key].rearrange("p (i c t u) -> p t i c u", i=NL, t=T, u=T)[:, t]
+                nc.vector.scalar_tensor_tensor(
+                    out=cols_t,
+                    in0=ones_q.rearrange("p (c u) -> p c u", u=T).unsqueeze(1).to_broadcast([P, NL, JG * NL, T]),
+                    scalar=sign,
+                    in1=cols_t,
+                    op0=ALU.mult,
+                    op1=ALU.add,
+                )
+
+        parts = {}
+        for key in ("var", "mean"):
+            for b in range(B):
+                parts[key, b] = const.tile([P, GROUPS, 4, PART], BF16, name="parts_%s%d" % (key, b))
+
+        def child_view(values, g):
+            return values.rearrange("p (i q m g) -> p g q i m", i=NL, q=JGROUPS, g=G)[:, g]
+
+        def part_view(key, b, g, part):
+            ap = parts[key, b][:, g * JGROUPS : (g + 1) * JGROUPS, part, :]
+            return ap.rearrange("p q (i m) -> p q i m", i=NL)
+
+        def child_parts():
+            var1 = const.tile([P, B, W_GAUSS], F32, name="var1")
+            nc.scalar.activation(out=var1, in_=log_std1, func=ACT.Exp, scale=2.0)
+            for b in range(B):
+                nc.vector.memset(parts["mean", b][:, :, 1, :], 0.0)
+                for g in range(G):
+                    nc.vector.tensor_copy(out=part_view("var", b, g, 0), in_=child_view(var1[:, b], g))
+                    nc.vector.tensor_tensor(
+                        out=part_view("var", b, g, 1),
+                        in0=child_view(var1[:, b], g),
+                        in1=part_view("var", b, g, 0),
+                        op=ALU.subtract,
+                    )
+                    nc.vector.tensor_copy(out=part_view("mean", b, g, 0), in_=child_view(mean1[:, b], g))
 
         bias = {}
 
@@ -89,13 +159,13 @@ def tile_chainlveg_pb_k_kernel(
 
         def transpose_x(n):
             cols = X_PASSES * K_PASS
-            x_raw = big.tile([P, B * cols], BF16, name="x_raw", tag="half", align_bytes=64)
+            x_raw = raw.tile([P, B * cols], BF16, name="x_raw", tag="raw", align_bytes=64)
             nc.sync.dma_start(
                 out=x_raw.rearrange("r (b k) -> r b k", b=B),
                 in_=x_next[:, :, n * cols : (n + 1) * cols].rearrange("b r k -> r b k"),
             )
             words = x_raw.bitcast(F32).rearrange("r (b c p u) -> r b c u p", b=B, c=X_PASSES, u=2)
-            x_grouped = big.tile([P, CHUNK], BF16, name="x_grouped", tag="full", align_bytes=64)
+            x_grouped = regrouped.tile([P, CHUNK], BF16, name="x_grouped", tag="grouped", align_bytes=64)
             grouped_words = x_grouped.bitcast(F32).rearrange("p (c b r u) -> p c b r u", c=X_PASSES, b=B, u=2)
             for c in range(X_PASSES):
                 xt = psum_t.tile([P, B, 2, P], F32, name="xt", tag="xt")
@@ -111,13 +181,13 @@ def tile_chainlveg_pb_k_kernel(
 
         def regroup_weights(w, width, s, vector_passes):
             passes = CHUNK // (PACK * width)
-            w_raw = w_in.tile([P, CHUNK], BF16, name="w_raw")
+            w_raw = raw.tile([P, CHUNK], BF16, name="w_raw", tag="raw", align_bytes=64)
             rows = w[s * passes * K_PASS : (s + 1) * passes * K_PASS, :]
             nc.sync.dma_start(
                 out=w_raw.rearrange("p (c e) -> p c e", c=passes),
                 in_=rows.rearrange("(c p j) w -> p c (j w)", c=passes, j=PACK),
             )
-            w_grouped = w_mx.tile([P, CHUNK], BF16, name="w_grouped", align_bytes=64)
+            w_grouped = regrouped.tile([P, CHUNK], BF16, name="w_grouped", tag="grouped", align_bytes=64)
             src = w_raw.rearrange("p (c j v i) -> p c v j i", c=passes, j=PACK, i=4)
             dst = w_grouped.rearrange("p (c v i j) -> p c v j i", c=passes, i=4, j=PACK)
             for c in range(passes):
@@ -147,17 +217,7 @@ def tile_chainlveg_pb_k_kernel(
                         stop=(k_pass == K // K_PASS - 1),
                     )
 
-        def plane_views(child, parent, g, t):
-            c = child.rearrange("p (i j t g) -> p t g i j", i=NL, j=NL, t=T, g=G)[:, t, g]
-            q = parent.rearrange("p (j c g) -> p g j c", j=NL, c=KU, g=G)[:, g]
-            shape = [P, NL, NL, KU]
-            return c.unsqueeze(3).to_broadcast(shape), q.unsqueeze(1).to_broadcast(shape)
-
-        def as_plane(ap):
-            return ap.rearrange("p (i j c) -> p i j c", i=NL, j=NL)
-
-        def flat(ap):
-            return ap.rearrange("p t n -> p (t n)")
+        N_OUT = T * PLANE
 
         def parent_term(acc, key):
             term = const.tile([P, B, W_GAUSS], F32, name="parent_" + key)
@@ -166,80 +226,82 @@ def tile_chainlveg_pb_k_kernel(
             nc.vector.tensor_scalar(out=term, in0=term, scalar1=CLIP, scalar2=-CLIP, op0=ALU.min, op1=ALU.max)
             return term
 
-        log_sum, precision, square, partial, result = {}, {}, {}, {}, {}
-        parent = {}
+        stationary = {}
 
-        def sum_of_variances(pair):
+        def turn_parts(key, b, term):
+            values = term[:, b].rearrange("p (q w g) -> p g q w", q=JGROUPS, g=G)
+            high = parts[key, b][:, :, 2, :].rearrange("p (g q) w -> p g q w", g=G)
+            low = parts[key, b][:, :, 3, :].rearrange("p (g q) w -> p g q w", g=G)
+            nc.vector.tensor_copy(out=high, in_=values)
+            nc.vector.tensor_tensor(out=low, in0=values, in1=high, op=ALU.subtract)
+            turned = psum_t.tile([P, GROUPS, P], BF16, name="turned", tag="xt")
+            for q in range(GROUPS):
+                nc.tensor.transpose(
+                    out=turned[:, q, :],
+                    in_=parts[key, b][:, q].rearrange("p a w -> p (a w)"),
+                    identity=ident_b,
+                )
+            stationary[key, b] = const.tile([P, GROUPS, P], BF16, name="stationary_%s%d" % (key, b))
+            nc.scalar.copy(out=stationary[key, b], in_=turned)
+
+        def pair_sums(key, b, q):
+            sums = psum_t.tile([P, GCOLS], F32, name="sums", tag="xt")
+            nc.tensor.matmul(out=sums, lhsT=stationary[key, b][:, q, :], rhs=spread[key], start=True, stop=True)
+            return sums.rearrange("p (i m) -> p i m", i=NL)
+
+        def group_cols(tile_g, q):
+            return tile_g.rearrange("p (i q m) -> p q i m", i=NL, q=JGROUPS)[:, q]
+
+        root, score = {}, {}
+
+        def inverse_root(pair):
             b, g = divmod(pair, G)
             if g == 0:
-                log_sum[b] = big.tile([P, G, T, PLANE], F32, name="log_sum", tag="full", align_bytes=64)
-            for t in range(T):
-                c, q = plane_views(var1[:, b], parent["var"][:, b], g, t)
-                nc.vector.tensor_tensor(out=as_plane(log_sum[b][:, g, t]), in0=c, in1=q, op=ALU.add)
+                root[b] = roots.tile([P, G, N_OUT], F32, name="root", align_bytes=64)
+            for q in range(JGROUPS):
+                nc.scalar.activation(
+                    out=group_cols(root[b][:, g], q),
+                    in_=pair_sums("var", b, g * JGROUPS + q),
+                    func=ACT.Abs_reciprocal_sqrt,
+                )
 
-        def log_of_sum(pair):
-            b, g = divmod(pair, G)
-            nc.scalar.activation(out=log_sum[b][:, g], in_=log_sum[b][:, g], func=ACT.Ln)
+        def product_of_roots(b):
+            score[b] = raw.tile([P, N_OUT], F32, name="score", tag="raw", align_bytes=64)
+            nc.vector.tensor_tensor(out=score[b], in0=root[b][:, 0], in1=root[b][:, 1], op=ALU.mult)
 
-        def one_over_sum(pair):
-            b, g = divmod(pair, G)
-            if g == 0:
-                precision[b] = big.tile([P, G, T, PLANE], F32, name="precision", tag="full", align_bytes=64)
-            nc.scalar.activation(out=precision[b][:, g], in_=log_sum[b][:, g], func=ACT.Exp, scale=-1.0)
+        def log_of_product(b):
+            nc.scalar.activation(out=score[b], in_=score[b], func=ACT.Ln)
 
-        def log_terms(pair):
-            b, g = divmod(pair, G)
-            if g == 0:
-                partial[b] = big.tile([P, T, PLANE], F32, name="partial", tag="half", align_bytes=64)
-            for t in range(T):
-                so_far = partial[b][:, t].rearrange("p (n c) -> p n c", c=KU)
-                if g == 0:
-                    before = weight1_here[:, b].rearrange("p (n t) -> p t n", t=T)[:, t]
-                    before = before.unsqueeze(2).to_broadcast([P, NL * NL, KU])
-                else:
-                    before = so_far
+        def log_terms(b):
+            for k in range(NL):
+                view = score[b].rearrange("p (n k c) -> p k n c", n=NL * NL, k=NL)[:, k]
                 nc.vector.scalar_tensor_tensor(
-                    out=so_far,
-                    in0=log_sum[b][:, g, t].rearrange("p (n c) -> p n c", c=KU),
-                    scalar=minus_half[:, b : b + 1],
-                    in1=before,
+                    out=view,
+                    in0=view,
+                    scalar=both[:, b : b + 1],
+                    in1=weight1_here[:, b].rearrange("p n t u -> p n (t u)"),
                     op0=ALU.mult,
                     op1=ALU.add,
                 )
 
-        def difference(pair):
+        def weighed_difference(pair):
             b, g = divmod(pair, G)
-            if g == 0:
-                square[b] = big.tile([P, G, T, PLANE], F32, name="square", tag="full", align_bytes=64)
-            for t in range(T):
-                c, q = plane_views(mean1[:, b], parent["mean"][:, b], g, t)
-                nc.vector.tensor_tensor(out=as_plane(square[b][:, g, t]), in0=c, in1=q, op=ALU.subtract)
+            for q in range(JGROUPS):
+                nc.vector.tensor_tensor(
+                    out=group_cols(root[b][:, g], q),
+                    in0=pair_sums("mean", b, g * JGROUPS + q),
+                    in1=group_cols(root[b][:, g], q),
+                    op=ALU.mult,
+                )
 
         def square_difference(pair):
             b, g = divmod(pair, G)
-            nc.scalar.activation(out=square[b][:, g], in_=square[b][:, g], func=ACT.Square)
+            nc.scalar.activation(out=root[b][:, g], in_=root[b][:, g], func=ACT.Square)
 
-        def weigh(pair):
+        def add_square(pair):
             b, g = divmod(pair, G)
             nc.vector.scalar_tensor_tensor(
-                out=flat(square[b][:, g]),
-                in0=flat(square[b][:, g]),
-                scalar=minus_half[:, b : b + 1],
-                in1=flat(precision[b][:, g]),
-                op0=ALU.mult,
-                op1=ALU.mult,
-            )
-
-        def sum_up(b):
-            nc.vector.tensor_tensor(
-                out=flat(square[b][:, 0]), in0=flat(square[b][:, 0]), in1=flat(square[b][:, 1]), op=ALU.add
-            )
-            result[b] = big.tile([P, T * PLANE], F32, name="result", tag="half", align_bytes=64)
-            nc.vector.tensor_tensor(
-                out=result[b].rearrange("p (n t u) -> p n t u", t=T, u=T),
-                in0=square[b][:, 0].rearrange("p t (n u) -> p n t u", u=T),
-                in1=partial[b].rearrange("p t (n u) -> p n t u", u=T),
-                op=ALU.add,
+                out=score[b], in0=root[b][:, g], scalar=minus_half[:, b : b + 1], in1=score[b], op0=ALU.mult, op1=ALU.add
             )
 
         def add_transition_weight(b, acc):
@@ -254,28 +316,34 @@ def tile_chainlveg_pb_k_kernel(
                 op0=ALU.add,
                 op1=ALU.mult,
             )
-            rows = result[b].rearrange("p (i m) -> p i m", i=NL)
-            nc.vector.tensor_tensor(
-                out=rows,
-                in0=rows,
-                in1=tw_t.rearrange("p n t u -> p (n t u)").unsqueeze(1).to_broadcast([P, NL, NL * NL * T * T]),
-                op=ALU.add,
-            )
-            nc.sync.dma_start(out=out[b].rearrange("p i j k t e u -> p (i j k t e u)"), in_=result[b])
+            result = score[b].rearrange("p (i m) -> p i m", i=NL)
+            rows = out[b].rearrange("p i j k t e u -> p i (j k t e u)")
+            for h in range(HALVES):
+                half = slice(h * NL // HALVES, (h + 1) * NL // HALVES)
+                nc.vector.tensor_tensor(
+                    out=result[:, half],
+                    in0=result[:, half],
+                    in1=tw_t.rearrange("p n t u -> p (n t u)")
+                    .unsqueeze(1)
+                    .to_broadcast([P, NL // HALVES, NL * NL * T * T]),
+                    op=ALU.add,
+                )
+                nc.sync.dma_start(out=rows[:, half], in_=result[:, half])
 
         streams = (
-            ("var", tpv_w, W_GAUSS, 3),
-            ("mean", tpm_w, W_GAUSS, 2),
-            ("weight", tw_w, W_WEIGHT, 0),
+            ("var", tpv_w, W_GAUSS, (3, 2)),
+            ("mean", tpm_w, W_GAUSS, (0, 4, 4, 4, 4, 2, 2, 2)),
+            ("weight", tw_w, W_WEIGHT, (1,)),
         )
         pieces = []
         for key, w, width, vector_passes in streams:
             for s in range(K * width // (P * CHUNK)):
-                pieces.append((key, w, width, vector_passes, s))
+                pieces.append((key, w, width, vector_passes[s % len(vector_passes)], s))
         var_done = K * W_GAUSS // (P * CHUNK)
         mean_done = 2 * var_done
         pairs = B * G
 
+        parent = {}
         acc = {}
         grouped = {}
         x_grouped = {}
@@ -283,16 +351,17 @@ def tile_chainlveg_pb_k_kernel(
             v = n - var_done - 1
             m = n - mean_done - 1
             if 0 <= v < pairs:
-                log_of_sum(v)
-            if pairs <= v < 2 * pairs:
-                one_over_sum(v - pairs)
-            if 0 <= m < pairs:
-                square_difference(m)
+                inverse_root(v)
+            if pairs <= v < pairs + B:
+                log_of_product(v - pairs)
             if n < X_CHUNKS:
                 x_grouped[n] = transpose_x(n)
             if n < len(pieces):
                 key, w, width, vector_passes, s = pieces[n]
                 grouped[n] = regroup_weights(w, width, s, vector_passes)
+            if n == 3:
+                child_parts()
+                child_weights()
             if n == X_CHUNKS - 1:
                 load_biases()
             if 1 <= n <= X_CHUNKS:
@@ -303,22 +372,21 @@ def tile_chainlveg_pb_k_kernel(
                     acc[key] = [psum_acc.tile([P, width], F32, name="acc", tag="acc%d" % b) for b in range(B)]
                 quantise_and_multiply(grouped[n - 1], width, s, acc[key])
             if n == var_done:
-                parent["log_std"] = parent_term(acc["var"], "var")
-                parent["var"] = const.tile([P, B, W_GAUSS], F32, name="var2")
-                nc.scalar.activation(out=parent["var"], in_=parent["log_std"], func=ACT.Exp, scale=2.0)
-                sum_of_variances(0)
-            if 0 <= v < pairs - 1:
-                sum_of_variances(v + 1)
-            if pairs <= v < 2 * pairs:
+                parent["var"] = parent_term(acc["var"], "var")
+                nc.scalar.activation(out=parent["var"], in_=parent["var"], func=ACT.Exp, scale=2.0)
+                for b in range(B):
+                    turn_parts("var", b, parent["var"])
+            if 1 <= v < pairs and v % G == G - 1:
+                product_of_roots(v // G)
+            if pairs <= v < pairs + B:
                 log_terms(v - pairs)
             if n == mean_done:
                 parent["mean"] = parent_term(acc["mean"], "mean")
-                difference(0)
-            if 0 <= m < pairs - 1:
-                difference(m + 1)
+                for b in range(B):
+                    turn_parts("mean", b, parent["mean"])
             if 0 <= m < pairs:
-                weigh(m)
-                if m % G == G - 1:
-                    sum_up(m // G)
+                weighed_difference(m)
+                square_difference(m)
+                add_square(m)
         for b in range(B):
             add_transition_weight(b, acc["weight"])

@@ -27,6 +27,8 @@ JG = 2
 JGROUPS = NL // JG
 PART = NL * JG * T
 GROUPS = G * JGROUPS
+LOAD_PARTS = {0: 2, 1: 2}
+AHEAD = 3
 HALVES = 2
 GCOLS = NL * JG * NL * T * T
 
@@ -44,6 +46,7 @@ def tile_chainlveg_pb_k_kernel(
 ):
     nc = tc.nc
     with ExitStack() as stack:
+        stack.enter_context(tc.manual_schedule())
         const = stack.enter_context(tc.tile_pool(name="const", bufs=1))
         raw = stack.enter_context(tc.tile_pool(name="raw", bufs=8))
         regrouped = stack.enter_context(tc.tile_pool(name="regrouped", bufs=5))
@@ -58,24 +61,30 @@ def tile_chainlveg_pb_k_kernel(
         make_identity(nc, ident_b)
 
         mean1 = const.tile([P, B, W_GAUSS], BF16, name="mean1")
-        nc.scalar.dma_start(out=mean1, in_=cs_mu.rearrange("b p i j t e g -> p b (i j t e g)"))
         log_std1 = const.tile([P, B, W_GAUSS], BF16, name="log_std1")
-        nc.scalar.dma_start(out=log_std1, in_=cs_var.rearrange("b p i j t e g -> p b (i j t e g)"))
         weight1 = const.tile([P, B, W_WEIGHT], BF16, name="weight1")
-        nc.scalar.dma_start(out=weight1, in_=cs_scale.rearrange("b p i j t e -> p b (i j t e)"))
+
+        def load_child():
+            nc.sync.dma_start(out=log_std1, in_=cs_var.rearrange("b p i j t e g -> p b (i j t e g)"))
+            nc.sync.dma_start(out=mean1, in_=cs_mu.rearrange("b p i j t e g -> p b (i j t e g)"))
+
+        def load_small():
+            nc.sync.dma_start(out=weight1, in_=cs_scale.rearrange("b p i j t e -> p b (i j t e)"))
+            nc.sync.dma_start(out=mask_rows[0:B, :], in_=mask_here)
+            nc.sync.dma_start(out=mask_rows[B : 2 * B, :], in_=mask_next)
 
         mask_rows = const.tile([P, P], BF16, name="mask_rows")
         nc.vector.memset(mask_rows, 0.0)
-        nc.scalar.dma_start(out=mask_rows[0:B, :], in_=mask_here)
-        nc.scalar.dma_start(out=mask_rows[B : 2 * B, :], in_=mask_next)
-        mask_cols = psum_t.tile([P, P], BF16, name="mask_cols", tag="xt")
-        nc.tensor.transpose(out=mask_cols, in_=mask_rows, identity=ident_b)
         factors = const.tile([P, 2 * B], F32, name="factors")
-        nc.vector.tensor_copy(out=factors, in_=mask_cols[:, 0 : 2 * B])
         both = const.tile([P, B], F32, name="both")
-        nc.vector.tensor_tensor(out=both, in0=factors[:, 0:B], in1=factors[:, B : 2 * B], op=ALU.mult)
         minus_half = const.tile([P, B], F32, name="minus_half")
-        nc.vector.tensor_scalar(out=minus_half, in0=both, scalar1=-0.5, scalar2=None, op0=ALU.mult)
+
+        def turn_masks():
+            mask_cols = psum_t.tile([P, P], BF16, name="mask_cols", tag="xt")
+            nc.tensor.transpose(out=mask_cols, in_=mask_rows, identity=ident_b)
+            nc.vector.tensor_copy(out=factors, in_=mask_cols[:, 0 : 2 * B])
+            nc.vector.tensor_tensor(out=both, in0=factors[:, 0:B], in1=factors[:, B : 2 * B], op=ALU.mult)
+            nc.vector.tensor_scalar(out=minus_half, in0=both, scalar1=-0.5, scalar2=None, op0=ALU.mult)
 
         weight1_here = const.tile([P, B, NL * NL, T, T], F32, name="weight1_here")
 
@@ -132,20 +141,27 @@ def tile_chainlveg_pb_k_kernel(
             ap = parts[key, b][:, g * JGROUPS : (g + 1) * JGROUPS, part, :]
             return ap.rearrange("p q (i m) -> p q i m", i=NL)
 
-        def child_parts():
-            var1 = const.tile([P, B, W_GAUSS], F32, name="var1")
-            nc.scalar.activation(out=var1, in_=log_std1, func=ACT.Exp, scale=2.0)
+        var1 = const.tile([P, B, W_GAUSS], F32, name="var1")
+        child_sets = [(b, g) for b in range(B) for g in range(G)]
+
+        def mean_child_parts():
             for b in range(B):
                 nc.vector.memset(parts["mean", b][:, :, 1, :], 0.0)
-                for g in range(G):
-                    nc.vector.tensor_copy(out=part_view("var", b, g, 0), in_=child_view(var1[:, b], g))
-                    nc.vector.tensor_tensor(
-                        out=part_view("var", b, g, 1),
-                        in0=child_view(var1[:, b], g),
-                        in1=part_view("var", b, g, 0),
-                        op=ALU.subtract,
-                    )
-                    nc.vector.tensor_copy(out=part_view("mean", b, g, 0), in_=child_view(mean1[:, b], g))
+            for b, g in child_sets:
+                nc.vector.tensor_copy(out=part_view("mean", b, g, 0), in_=child_view(mean1[:, b], g))
+
+        def var_child_high_parts():
+            for b, g in child_sets:
+                nc.vector.tensor_copy(out=part_view("var", b, g, 0), in_=child_view(var1[:, b], g))
+
+        def var_child_low_parts():
+            for b, g in child_sets:
+                nc.vector.tensor_tensor(
+                    out=part_view("var", b, g, 1),
+                    in0=child_view(var1[:, b], g),
+                    in1=part_view("var", b, g, 0),
+                    op=ALU.subtract,
+                )
 
         bias = {}
 
@@ -157,13 +173,21 @@ def tile_chainlveg_pb_k_kernel(
         x_codes = const.tile([P, K // K_PASS * B * P], U32, name="x_codes", align_bytes=64)
         x_scales = const.tile([P, K // K_PASS * B * P], U8, name="x_scales", align_bytes=64)
 
-        def transpose_x(n):
+        x_raws, w_raws = {}, {}
+        acc, grouped, pieces = {}, {}, []
+
+        def load_x(n, part, parts_of):
             cols = X_PASSES * K_PASS
-            x_raw = raw.tile([P, B * cols], BF16, name="x_raw", tag="raw", align_bytes=64)
+            if part == 0:
+                x_raws[n] = raw.tile([P, B * cols], BF16, name="x_raw", tag="raw", align_bytes=64)
+            k = slice(part * cols // parts_of, (part + 1) * cols // parts_of)
             nc.sync.dma_start(
-                out=x_raw.rearrange("r (b k) -> r b k", b=B),
-                in_=x_next[:, :, n * cols : (n + 1) * cols].rearrange("b r k -> r b k"),
+                out=x_raws[n].rearrange("r (b k) -> r b k", b=B)[:, :, k],
+                in_=x_next[:, :, n * cols : (n + 1) * cols].rearrange("b r k -> r b k")[:, :, k],
             )
+
+        def transpose_x(n):
+            x_raw = x_raws[n]
             words = x_raw.bitcast(F32).rearrange("r (b c p u) -> r b c u p", b=B, c=X_PASSES, u=2)
             x_grouped = regrouped.tile([P, CHUNK], BF16, name="x_grouped", tag="grouped", align_bytes=64)
             grouped_words = x_grouped.bitcast(F32).rearrange("p (c b r u) -> p c b r u", c=X_PASSES, b=B, u=2)
@@ -179,36 +203,59 @@ def tile_chainlveg_pb_k_kernel(
             cols = slice(n * CHUNK // PACK, (n + 1) * CHUNK // PACK)
             nc.vector.quantize_mx(out=x_codes[:, cols].bitcast(FP8X4), scales=x_scales[:, cols], in_=x_grouped)
 
-        def regroup_weights(w, width, s, vector_passes):
+        def load_weights(n, w, width, s, part, parts_of):
             passes = CHUNK // (PACK * width)
-            w_raw = raw.tile([P, CHUNK], BF16, name="w_raw", tag="raw", align_bytes=64)
+            if part == 0:
+                w_raws[n] = raw.tile([P, CHUNK], BF16, name="w_raw", tag="raw", align_bytes=64)
             rows = w[s * passes * K_PASS : (s + 1) * passes * K_PASS, :]
+            c = slice(part * passes // parts_of, (part + 1) * passes // parts_of)
             nc.sync.dma_start(
-                out=w_raw.rearrange("p (c e) -> p c e", c=passes),
-                in_=rows.rearrange("(c p j) w -> p c (j w)", c=passes, j=PACK),
+                out=w_raws[n].rearrange("p (c e) -> p c e", c=passes)[:, c],
+                in_=rows.rearrange("(c p j) w -> p c (j w)", c=passes, j=PACK)[:, c],
             )
-            w_grouped = regrouped.tile([P, CHUNK], BF16, name="w_grouped", tag="grouped", align_bytes=64)
-            src = w_raw.rearrange("p (c j v i) -> p c v j i", c=passes, j=PACK, i=4)
-            dst = w_grouped.rearrange("p (c v i j) -> p c v j i", c=passes, i=4, j=PACK)
-            for c in range(passes):
-                if c < vector_passes:
-                    nc.vector.tensor_copy(out=dst[:, c], in_=src[:, c])
-                else:
-                    nc.scalar.copy(out=dst[:, c], in_=src[:, c])
-            return w_grouped
 
-        def quantise_and_multiply(w_grouped, width, s, acc):
+        def regroup_views(n, width):
             passes = CHUNK // (PACK * width)
-            w_codes = w_mx.tile([P, CHUNK // PACK], U32, name="w_codes", align_bytes=64)
-            w_scales = w_mx.tile([P, CHUNK // PACK], U8, name="w_scales", align_bytes=64)
-            nc.vector.quantize_mx(out=w_codes.bitcast(FP8X4), scales=w_scales, in_=w_grouped)
+            src = w_raws[n].rearrange("p (c j v i) -> p c v j i", c=passes, j=PACK, i=4)
+            dst = grouped[n].rearrange("p (c v i j) -> p c v j i", c=passes, i=4, j=PACK)
+            return src, dst, passes
+
+        def regroup_on_vector(n):
+            key, w, width, vector_passes, s = pieces[n]
+            grouped[n] = regrouped.tile([P, CHUNK], BF16, name="w_grouped", tag="grouped", align_bytes=64)
+            src, dst, passes = regroup_views(n, width)
+            for c in range(0, vector_passes, 2):
+                pair = slice(c, min(c + 2, vector_passes))
+                nc.vector.tensor_copy(out=dst[:, pair], in_=src[:, pair])
+
+        def regroup_on_scalar(n):
+            key, w, width, vector_passes, s = pieces[n]
+            src, dst, passes = regroup_views(n, width)
+            if vector_passes < passes:
+                nc.scalar.copy(out=dst[:, vector_passes:], in_=src[:, vector_passes:])
+
+        codes = {}
+
+        def quantise_weights(n):
+            codes[n] = (
+                w_mx.tile([P, CHUNK // PACK], U32, name="w_codes", align_bytes=64),
+                w_mx.tile([P, CHUNK // PACK], U8, name="w_scales", align_bytes=64),
+            )
+            nc.vector.quantize_mx(out=codes[n][0].bitcast(FP8X4), scales=codes[n][1], in_=grouped[n])
+
+        def multiply(n):
+            key, w, width, vector_passes, s = pieces[n]
+            passes = CHUNK // (PACK * width)
+            if s == 0:
+                acc[key] = [psum_acc.tile([P, width], F32, name="acc", tag="acc%d" % b) for b in range(B)]
+            w_codes, w_scales = codes[n]
             for c in range(passes):
                 k_pass = s * passes + c
                 w_cols = slice(c * width, (c + 1) * width)
                 for b in range(B):
                     x_cols = slice((k_pass * B + b) * P, (k_pass * B + b + 1) * P)
                     nc.tensor.matmul_mx(
-                        out=acc[b],
+                        out=acc[key][b],
                         lhsT=x_codes[:, x_cols].bitcast(FP8X4),
                         lhsT_scale=x_scales[:, x_cols],
                         rhs=w_codes[:, w_cols].bitcast(FP8X4),
@@ -228,12 +275,14 @@ def tile_chainlveg_pb_k_kernel(
 
         stationary = {}
 
-        def turn_parts(key, b, term):
+        def split_parent(key, b, term):
             values = term[:, b].rearrange("p (q w g) -> p g q w", q=JGROUPS, g=G)
             high = parts[key, b][:, :, 2, :].rearrange("p (g q) w -> p g q w", g=G)
             low = parts[key, b][:, :, 3, :].rearrange("p (g q) w -> p g q w", g=G)
             nc.vector.tensor_copy(out=high, in_=values)
             nc.vector.tensor_tensor(out=low, in0=values, in1=high, op=ALU.subtract)
+
+        def turn_parts(key, b):
             turned = psum_t.tile([P, GROUPS, P], BF16, name="turned", tag="xt")
             for q in range(GROUPS):
                 nc.tensor.transpose(
@@ -254,11 +303,11 @@ def tile_chainlveg_pb_k_kernel(
 
         root, score = {}, {}
 
-        def inverse_root(pair):
+        def inverse_root(pair, qs=range(JGROUPS)):
             b, g = divmod(pair, G)
-            if g == 0:
+            if b not in root:
                 root[b] = roots.tile([P, G, N_OUT], F32, name="root", align_bytes=64)
-            for q in range(JGROUPS):
+            for q in qs:
                 nc.scalar.activation(
                     out=group_cols(root[b][:, g], q),
                     in_=pair_sums("var", b, g * JGROUPS + q),
@@ -304,9 +353,11 @@ def tile_chainlveg_pb_k_kernel(
                 out=score[b], in0=root[b][:, g], scalar=minus_half[:, b : b + 1], in1=score[b], op0=ALU.mult, op1=ALU.add
             )
 
-        def add_transition_weight(b, acc):
+        tw_terms = {}
+
+        def transition_weight(b, acc):
             tw = const.tile([P, W_WEIGHT], F32, name="tw%d" % b)
-            nc.vector.tensor_tensor(out=tw, in0=acc[b], in1=bias["weight"], op=ALU.add)
+            nc.vector.tensor_tensor(out=tw, in0=acc, in1=bias["weight"], op=ALU.add)
             tw_t = const.tile([P, NL * NL, T, T], F32, name="tw_t%d" % b)
             nc.vector.tensor_scalar(
                 out=tw_t,
@@ -316,6 +367,10 @@ def tile_chainlveg_pb_k_kernel(
                 op0=ALU.add,
                 op1=ALU.mult,
             )
+            tw_terms[b] = tw_t
+
+        def add_transition_weight(b):
+            tw_t = tw_terms[b]
             result = score[b].rearrange("p (i m) -> p i m", i=NL)
             rows = out[b].rearrange("p i j k t e u -> p i (j k t e u)")
             for h in range(HALVES):
@@ -332,61 +387,153 @@ def tile_chainlveg_pb_k_kernel(
 
         streams = (
             ("var", tpv_w, W_GAUSS, (3, 2)),
-            ("mean", tpm_w, W_GAUSS, (0, 4, 4, 4, 4, 2, 2, 2)),
-            ("weight", tw_w, W_WEIGHT, (1,)),
+            ("mean", tpm_w, W_GAUSS, (0, 2, 4, 4, 4, 4, 2, 2)),
+            ("weight", tw_w, W_WEIGHT, (0,)),
         )
-        pieces = []
         for key, w, width, vector_passes in streams:
             for s in range(K * width // (P * CHUNK)):
                 pieces.append((key, w, width, vector_passes[s % len(vector_passes)], s))
         var_done = K * W_GAUSS // (P * CHUNK)
         mean_done = 2 * var_done
-        pairs = B * G
+        last = len(pieces) - 1
 
         parent = {}
-        acc = {}
-        grouped = {}
+
+        def load(n):
+            if n > last:
+                return
+            key, w, width, vector_passes, s = pieces[n]
+            parts_of = LOAD_PARTS.get(n, 1)
+            for part in range(parts_of):
+                if n < X_CHUNKS:
+                    load_x(n, part, parts_of)
+                load_weights(n, w, width, s, part, parts_of)
+
+        load(0)
+        load(1)
+        load_child()
+        for n in range(2, AHEAD):
+            load(n)
+        load_small()
         x_grouped = {}
-        for n in range(len(pieces) + 1):
-            v = n - var_done - 1
-            m = n - mean_done - 1
-            if 0 <= v < pairs:
-                inverse_root(v)
-            if pairs <= v < pairs + B:
-                log_of_product(v - pairs)
-            if n < X_CHUNKS:
-                x_grouped[n] = transpose_x(n)
-            if n < len(pieces):
-                key, w, width, vector_passes, s = pieces[n]
-                grouped[n] = regroup_weights(w, width, s, vector_passes)
+
+        def regroup(n):
+            load(n + AHEAD)
+            if n <= last:
+                regroup_on_vector(n)
+                regroup_on_scalar(n)
+
+        for n in range(X_CHUNKS):
+            x_grouped[n] = transpose_x(n)
+            regroup(n)
+            if n == 2:
+                nc.scalar.activation(out=var1, in_=log_std1, func=ACT.Exp, scale=2.0)
+                mean_child_parts()
             if n == 3:
-                child_parts()
+                var_child_high_parts()
+            if n == 4:
+                var_child_low_parts()
+            if n == 5:
+                turn_masks()
                 child_weights()
-            if n == X_CHUNKS - 1:
+            if n == var_done - 2:
                 load_biases()
-            if 1 <= n <= X_CHUNKS:
-                quantise_x(n - 1, x_grouped[n - 1])
             if n >= 1:
-                key, w, width, vector_passes, s = pieces[n - 1]
-                if s == 0:
-                    acc[key] = [psum_acc.tile([P, width], F32, name="acc", tag="acc%d" % b) for b in range(B)]
-                quantise_and_multiply(grouped[n - 1], width, s, acc[key])
-            if n == var_done:
-                parent["var"] = parent_term(acc["var"], "var")
-                nc.scalar.activation(out=parent["var"], in_=parent["var"], func=ACT.Exp, scale=2.0)
-                for b in range(B):
-                    turn_parts("var", b, parent["var"])
-            if 1 <= v < pairs and v % G == G - 1:
-                product_of_roots(v // G)
-            if pairs <= v < pairs + B:
-                log_terms(v - pairs)
-            if n == mean_done:
-                parent["mean"] = parent_term(acc["mean"], "mean")
-                for b in range(B):
-                    turn_parts("mean", b, parent["mean"])
-            if 0 <= m < pairs:
-                weighed_difference(m)
-                square_difference(m)
-                add_square(m)
+                quantise_x(n - 1, x_grouped[n - 1])
+                quantise_weights(n - 1)
+            if n >= 2:
+                multiply(n - 2)
+        sv, ss, q, mx = regroup_on_vector, regroup_on_scalar, quantise_weights, multiply
+
+        def prefetch(n):
+            load(n + AHEAD)
+
+        def first_half(key):
+            parent[key] = parent_term(acc[key], key)
+            if key == "var":
+                nc.scalar.activation(out=parent[key], in_=parent[key], func=ACT.Exp, scale=2.0)
+
+        def second_half(key):
+            for b in range(B):
+                split_parent(key, b, parent[key])
+            for b in range(B):
+                turn_parts(key, b)
+
+        def differences(m):
+            weighed_difference(m)
+            square_difference(m)
+
+        n = var_done
+        prefetch(n)
+        sv(n)
+        ss(n)
+        quantise_x(n - 1, x_grouped[n - 1])
+        q(n - 1)
+        mx(n - 2)
+        mx(n - 1)
+        prefetch(n + 1)
+        sv(n + 1)
+        ss(n + 1)
+        first_half("var")
+        q(n)
+        second_half("var")
+        mx(n)
+        for r in range(4):
+            inverse_root(r)
+            prefetch(n + 2 + r)
+            sv(n + 2 + r)
+            ss(n + 2 + r)
+            q(n + 1 + r)
+            mx(n + 1 + r)
+        n = n + 6
+        product_of_roots(0)
+        prefetch(n)
+        sv(n)
+        ss(n)
+        q(n - 1)
+        mx(n - 1)
+        log_of_product(0)
+        n = n + 1
+        prefetch(n)
+        sv(n)
+        ss(n)
+        product_of_roots(1)
+        q(n - 1)
+        mx(n - 1)
+        n = n + 1
+        prefetch(n)
+        sv(n)
+        log_of_product(1)
+        q(n - 1)
+        mx(n - 1)
+        log_terms(0)
+        first_half("mean")
+        ss(n)
+        second_half("mean")
+        sv(n + 1)
+        log_terms(1)
+        ss(n + 1)
+        q(n)
+        differences(0)
+        differences(1)
+        sv(n + 2)
+        ss(n + 2)
+        mx(n)
+        q(n + 1)
+        mx(n + 1)
+        add_square(0)
+        sv(n + 3)
+        ss(n + 3)
+        differences(2)
+        differences(3)
+        q(n + 2)
+        mx(n + 2)
+        add_square(1)
+        q(n + 3)
+        mx(n + 3)
+        add_square(2)
         for b in range(B):
-            add_transition_weight(b, acc["weight"])
+            transition_weight(b, acc["weight"][b])
+        add_transition_weight(0)
+        add_square(3)
+        add_transition_weight(1)

@@ -386,8 +386,8 @@ def tile_chainlveg_pb_k_kernel(
                 nc.sync.dma_start(out=rows[:, half], in_=result[:, half])
 
         streams = (
-            ("var", tpv_w, W_GAUSS, (3, 2)),
-            ("mean", tpm_w, W_GAUSS, (0, 2, 4, 4, 4, 4, 2, 2)),
+            ("var", tpv_w, W_GAUSS, (3,)),
+            ("mean", tpm_w, W_GAUSS, (2, 2, 4, 4, 4, 4, 2, 2)),
             ("weight", tw_w, W_WEIGHT, (0,)),
         )
         for key, w, width, vector_passes in streams:
@@ -438,11 +438,10 @@ def tile_chainlveg_pb_k_kernel(
                 child_weights()
             if n == var_done - 2:
                 load_biases()
+            quantise_x(n, x_grouped[n])
+            quantise_weights(n)
             if n >= 1:
-                quantise_x(n - 1, x_grouped[n - 1])
-                quantise_weights(n - 1)
-            if n >= 2:
-                multiply(n - 2)
+                multiply(n - 1)
         sv, ss, q, mx = regroup_on_vector, regroup_on_scalar, quantise_weights, multiply
 
         def prefetch(n):
@@ -465,12 +464,9 @@ def tile_chainlveg_pb_k_kernel(
 
         n = var_done
         prefetch(n)
+        mx(n - 1)
         sv(n)
         ss(n)
-        quantise_x(n - 1, x_grouped[n - 1])
-        q(n - 1)
-        mx(n - 2)
-        mx(n - 1)
         prefetch(n + 1)
         sv(n + 1)
         ss(n + 1)

@@ -27,6 +27,7 @@ JG = 2
 JGROUPS = NL // JG
 PART = NL * JG * T
 GROUPS = G * JGROUPS
+RUN = 8
 LOAD_PARTS = {0: 2, 1: 2}
 AHEAD = 3
 HALVES = 2
@@ -216,8 +217,8 @@ def tile_chainlveg_pb_k_kernel(
 
         def regroup_views(n, width):
             passes = CHUNK // (PACK * width)
-            src = w_raws[n].rearrange("p (c j v i) -> p c v j i", c=passes, j=PACK, i=4)
-            dst = grouped[n].rearrange("p (c v i j) -> p c v j i", c=passes, i=4, j=PACK)
+            src = w_raws[n].rearrange("p (c j v i) -> p c v j i", c=passes, j=PACK, i=RUN)
+            dst = grouped[n].rearrange("p (c v i j) -> p c v j i", c=passes, i=RUN, j=PACK)
             return src, dst, passes
 
         def regroup_on_vector(n):

@@ -17,7 +17,6 @@ B = 2
 K = 16384
 NL, T, G = 8, 2, 2
 KU = NL * T
-PLANE = NL * NL * KU
 W_WEIGHT = NL * NL * T
 W_GAUSS = W_WEIGHT * G
 CLIP = 1.0
@@ -27,9 +26,14 @@ JG = 2
 JGROUPS = NL // JG
 PART = NL * JG * T
 GROUPS = G * JGROUPS
+NI = 2
+CHUNKS = NL // NI
+M = NI * JG * NL * T * T
+N_OUT = NL * NL * NL * T * T
+BIG = 16
 RUN = 8
 LOAD_PARTS = {0: 2, 1: 2}
-AHEAD = 3
+AHEAD = 4
 HALVES = 2
 GCOLS = NL * JG * NL * T * T
 
@@ -49,10 +53,8 @@ def tile_chainlveg_pb_k_kernel(
     with ExitStack() as stack:
         stack.enter_context(tc.manual_schedule())
         const = stack.enter_context(tc.tile_pool(name="const", bufs=1))
-        raw = stack.enter_context(tc.tile_pool(name="raw", bufs=8))
-        regrouped = stack.enter_context(tc.tile_pool(name="regrouped", bufs=5))
+        big = stack.enter_context(tc.tile_pool(name="big", bufs=BIG))
         w_mx = stack.enter_context(tc.tile_pool(name="w_mx", bufs=3))
-        roots = stack.enter_context(tc.tile_pool(name="roots", bufs=2))
         psum_t = stack.enter_context(tc.psum_pool(name="psum_t", bufs=4))
         psum_acc = stack.enter_context(tc.psum_pool(name="psum_acc", bufs=2))
 
@@ -89,6 +91,8 @@ def tile_chainlveg_pb_k_kernel(
 
         weight1_here = const.tile([P, B, NL * NL, T, T], F32, name="weight1_here")
 
+        child_term = [const.tile([P, N_OUT], F32, name="child_term%d" % b) for b in range(B)]
+
         def child_weights():
             for b in range(B):
                 nc.vector.tensor_scalar(
@@ -100,6 +104,13 @@ def tile_chainlveg_pb_k_kernel(
                     scalar1=factors[:, b : b + 1],
                     scalar2=None,
                     op0=ALU.mult,
+                )
+                nc.vector.tensor_copy(
+                    out=child_term[b].rearrange("p (n k c) -> p n k c", n=NL * NL, k=NL),
+                    in_=weight1_here[:, b]
+                    .rearrange("p n t u -> p n (t u)")
+                    .unsqueeze(2)
+                    .to_broadcast([P, NL * NL, NL, T * T]),
                 )
 
         ones_c = const.tile([P, PART], BF16, name="ones_c")
@@ -180,7 +191,7 @@ def tile_chainlveg_pb_k_kernel(
         def load_x(n, part, parts_of):
             cols = X_PASSES * K_PASS
             if part == 0:
-                x_raws[n] = raw.tile([P, B * cols], BF16, name="x_raw", tag="raw", align_bytes=64)
+                x_raws[n] = big.tile([P, B * cols], BF16, name="x_raw", tag="big", align_bytes=64)
             k = slice(part * cols // parts_of, (part + 1) * cols // parts_of)
             nc.sync.dma_start(
                 out=x_raws[n].rearrange("r (b k) -> r b k", b=B)[:, :, k],
@@ -190,7 +201,7 @@ def tile_chainlveg_pb_k_kernel(
         def transpose_x(n):
             x_raw = x_raws[n]
             words = x_raw.bitcast(F32).rearrange("r (b c p u) -> r b c u p", b=B, c=X_PASSES, u=2)
-            x_grouped = regrouped.tile([P, CHUNK], BF16, name="x_grouped", tag="grouped", align_bytes=64)
+            x_grouped = big.tile([P, CHUNK], BF16, name="x_grouped", tag="big", align_bytes=64)
             grouped_words = x_grouped.bitcast(F32).rearrange("p (c b r u) -> p c b r u", c=X_PASSES, b=B, u=2)
             for c in range(X_PASSES):
                 xt = psum_t.tile([P, B, 2, P], F32, name="xt", tag="xt")
@@ -207,7 +218,7 @@ def tile_chainlveg_pb_k_kernel(
         def load_weights(n, w, width, s, part, parts_of):
             passes = CHUNK // (PACK * width)
             if part == 0:
-                w_raws[n] = raw.tile([P, CHUNK], BF16, name="w_raw", tag="raw", align_bytes=64)
+                w_raws[n] = big.tile([P, CHUNK], BF16, name="w_raw", tag="big", align_bytes=64)
             rows = w[s * passes * K_PASS : (s + 1) * passes * K_PASS, :]
             c = slice(part * passes // parts_of, (part + 1) * passes // parts_of)
             nc.sync.dma_start(
@@ -217,13 +228,14 @@ def tile_chainlveg_pb_k_kernel(
 
         def regroup_views(n, width):
             passes = CHUNK // (PACK * width)
+            if n not in grouped:
+                grouped[n] = big.tile([P, CHUNK], BF16, name="w_grouped", tag="big", align_bytes=64)
             src = w_raws[n].rearrange("p (c j v i) -> p c v j i", c=passes, j=PACK, i=RUN)
             dst = grouped[n].rearrange("p (c v i j) -> p c v j i", c=passes, i=RUN, j=PACK)
             return src, dst, passes
 
         def regroup_on_vector(n):
             key, w, width, vector_passes, s = pieces[n]
-            grouped[n] = regrouped.tile([P, CHUNK], BF16, name="w_grouped", tag="grouped", align_bytes=64)
             src, dst, passes = regroup_views(n, width)
             for c in range(0, vector_passes, 2):
                 pair = slice(c, min(c + 2, vector_passes))
@@ -265,7 +277,6 @@ def tile_chainlveg_pb_k_kernel(
                         stop=(k_pass == K // K_PASS - 1),
                     )
 
-        N_OUT = T * PLANE
 
         def parent_term(acc, key):
             term = const.tile([P, B, W_GAUSS], F32, name="parent_" + key)
@@ -274,7 +285,7 @@ def tile_chainlveg_pb_k_kernel(
             nc.vector.tensor_scalar(out=term, in0=term, scalar1=CLIP, scalar2=-CLIP, op0=ALU.min, op1=ALU.max)
             return term
 
-        stationary = {}
+        turned = {}
 
         def split_parent(key, b, term):
             values = term[:, b].rearrange("p (q w g) -> p g q w", q=JGROUPS, g=G)
@@ -284,74 +295,82 @@ def tile_chainlveg_pb_k_kernel(
             nc.vector.tensor_tensor(out=low, in0=values, in1=high, op=ALU.subtract)
 
         def turn_parts(key, b):
-            turned = psum_t.tile([P, GROUPS, P], BF16, name="turned", tag="xt")
+            if key not in turned:
+                turned[key] = const.tile([P, GROUPS, B, P], BF16, name="turned_" + key)
+            in_psum = psum_t.tile([P, GROUPS, P], BF16, name="turned_psum", tag="xt")
             for q in range(GROUPS):
                 nc.tensor.transpose(
-                    out=turned[:, q, :],
+                    out=in_psum[:, q, :],
                     in_=parts[key, b][:, q].rearrange("p a w -> p (a w)"),
                     identity=ident_b,
                 )
-            stationary[key, b] = const.tile([P, GROUPS, P], BF16, name="stationary_%s%d" % (key, b))
-            nc.scalar.copy(out=stationary[key, b], in_=turned)
+            nc.scalar.copy(out=turned[key][:, :, b, :], in_=in_psum)
 
-        def pair_sums(key, b, q):
-            sums = psum_t.tile([P, GCOLS], F32, name="sums", tag="xt")
-            nc.tensor.matmul(out=sums, lhsT=stationary[key, b][:, q, :], rhs=spread[key], start=True, stop=True)
-            return sums.rearrange("p (i m) -> p i m", i=NL)
-
-        def group_cols(tile_g, q):
-            return tile_g.rearrange("p (i q m) -> p q i m", i=NL, q=JGROUPS)[:, q]
-
-        root, score = {}, {}
-
-        def inverse_root(pair, qs=range(JGROUPS)):
-            b, g = divmod(pair, G)
-            if b not in root:
-                root[b] = roots.tile([P, G, N_OUT], F32, name="root", align_bytes=64)
-            for q in qs:
-                nc.scalar.activation(
-                    out=group_cols(root[b][:, g], q),
-                    in_=pair_sums("var", b, g * JGROUPS + q),
-                    func=ACT.Abs_reciprocal_sqrt,
+        def pair_sums(key, ic, g, h):
+            sums = psum_t.tile([P, 2, B * P], F32, name="sums", tag="xt")
+            for l in range(2):
+                nc.tensor.matmul(
+                    out=sums[:, l, :],
+                    lhsT=spread[key][:, ic * M : (ic + 1) * M],
+                    rhs=turned[key][:, g * JGROUPS + 2 * h + l].rearrange("p b r -> p (b r)"),
+                    start=True,
+                    stop=True,
                 )
+            return sums
 
-        def product_of_roots(b):
-            score[b] = raw.tile([P, N_OUT], F32, name="score", tag="raw", align_bytes=64)
-            nc.vector.tensor_tensor(out=score[b], in0=root[b][:, 0], in1=root[b][:, 1], op=ALU.mult)
+        logs, root, result = {}, {}, {}
 
-        def log_of_product(b):
-            nc.scalar.activation(out=score[b], in_=score[b], func=ACT.Ln)
+        def log_of_sum(ic):
+            logs[ic] = big.tile([P, G, JGROUPS, B * P], F32, name="logs", tag="big", align_bytes=64)
+            for g in range(G):
+                for h in range(2):
+                    nc.scalar.activation(
+                        out=logs[ic][:, g, 2 * h : 2 * h + 2, :], in_=pair_sums("var", ic, g, h), func=ACT.Ln
+                    )
 
-        def log_terms(b):
-            for k in range(NL):
-                view = score[b].rearrange("p (n k c) -> p k n c", n=NL * NL, k=NL)[:, k]
-                nc.vector.scalar_tensor_tensor(
-                    out=view,
-                    in0=view,
-                    scalar=both[:, b : b + 1],
-                    in1=weight1_here[:, b].rearrange("p n t u -> p n (t u)"),
-                    op0=ALU.mult,
-                    op1=ALU.add,
-                )
+        def flat(tile4):
+            return tile4.rearrange("p g q n -> p (g q n)")
 
-        def weighed_difference(pair):
-            b, g = divmod(pair, G)
+        def inverse_root(ic):
+            root[ic] = big.tile([P, G, JGROUPS, B * P], F32, name="root", tag="big", align_bytes=64)
+            nc.scalar.activation(out=flat(root[ic]), in_=flat(logs[ic]), func=ACT.Exp, scale=-0.5)
+
+        def weighed_difference(ic):
+            for g in range(G):
+                for h in range(2):
+                    part = root[ic][:, g, 2 * h : 2 * h + 2, :]
+                    nc.vector.tensor_tensor(out=part, in0=pair_sums("mean", ic, g, h), in1=part, op=ALU.mult)
+
+        def square_difference(ic):
+            nc.scalar.activation(out=flat(root[ic]), in_=flat(root[ic]), func=ACT.Square)
+
+        def turn_back(ic, b):
+            total = psum_acc.tile([P, NI, JGROUPS, M // NI], F32, name="total", tag="acc%d" % b)
             for q in range(JGROUPS):
-                nc.vector.tensor_tensor(
-                    out=group_cols(root[b][:, g], q),
-                    in0=pair_sums("mean", b, g * JGROUPS + q),
-                    in1=group_cols(root[b][:, g], q),
-                    op=ALU.mult,
-                )
+                terms = [logs[ic][:, 0], logs[ic][:, 1], root[ic][:, 0], root[ic][:, 1]]
+                for k, term in enumerate(terms):
+                    nc.tensor.matmul(
+                        out=total[:, :, q, :],
+                        lhsT=term[:, q, b * P : (b + 1) * P],
+                        rhs=ident_f,
+                        start=(k == 0),
+                        stop=(k == len(terms) - 1),
+                        is_transpose=True,
+                    )
+            return total
 
-        def square_difference(pair):
-            b, g = divmod(pair, G)
-            nc.scalar.activation(out=root[b][:, g], in_=root[b][:, g], func=ACT.Square)
-
-        def add_square(pair):
-            b, g = divmod(pair, G)
+        def add_child_term(ic, b):
+            total = turn_back(ic, b)
+            if b not in result:
+                result[b] = big.tile([P, N_OUT], F32, name="result", tag="big", align_bytes=64)
+            cols = slice(ic * (N_OUT // CHUNKS), (ic + 1) * (N_OUT // CHUNKS))
             nc.vector.scalar_tensor_tensor(
-                out=score[b], in0=root[b][:, g], scalar=minus_half[:, b : b + 1], in1=score[b], op0=ALU.mult, op1=ALU.add
+                out=result[b][:, cols],
+                in0=total.rearrange("p i q m -> p (i q m)"),
+                scalar=minus_half[:, b : b + 1],
+                in1=child_term[b][:, cols],
+                op0=ALU.mult,
+                op1=ALU.add,
             )
 
         tw_terms = {}
@@ -370,26 +389,26 @@ def tile_chainlveg_pb_k_kernel(
             )
             tw_terms[b] = tw_t
 
-        def add_transition_weight(b):
-            tw_t = tw_terms[b]
-            result = score[b].rearrange("p (i m) -> p i m", i=NL)
-            rows = out[b].rearrange("p i j k t e u -> p i (j k t e u)")
-            for h in range(HALVES):
-                half = slice(h * NL // HALVES, (h + 1) * NL // HALVES)
-                nc.vector.tensor_tensor(
-                    out=result[:, half],
-                    in0=result[:, half],
-                    in1=tw_t.rearrange("p n t u -> p (n t u)")
-                    .unsqueeze(1)
-                    .to_broadcast([P, NL // HALVES, NL * NL * T * T]),
-                    op=ALU.add,
-                )
-                nc.sync.dma_start(out=rows[:, half], in_=result[:, half])
+        def add_transition_weight(ic, b):
+            rows = result[b].rearrange("p (i m) -> p i m", i=NL)[:, ic * NI : (ic + 1) * NI]
+            nc.vector.tensor_tensor(
+                out=rows,
+                in0=rows,
+                in1=tw_terms[b].rearrange("p n t u -> p (n t u)").unsqueeze(1).to_broadcast([P, NI, NL * NL * T * T]),
+                op=ALU.add,
+            )
+            store(ic, b)
+
+        def store(ic, b):
+            nc.sync.dma_start(
+                out=out[b].rearrange("p i j k t e u -> p i (j k t e u)")[:, ic * NI : (ic + 1) * NI],
+                in_=result[b].rearrange("p (i m) -> p i m", i=NL)[:, ic * NI : (ic + 1) * NI],
+            )
 
         streams = (
-            ("var", tpv_w, W_GAUSS, (3,)),
-            ("mean", tpm_w, W_GAUSS, (2, 2, 4, 4, 4, 4, 2, 2)),
-            ("weight", tw_w, W_WEIGHT, (0,)),
+            ("var", tpv_w, W_GAUSS, (2, 3)),
+            ("mean", tpm_w, W_GAUSS, (0, 2, 4, 4, 4, 4, 4, 4)),
+            ("weight", tw_w, W_WEIGHT, (2, 4, 6, 6)),
         )
         for key, w, width, vector_passes in streams:
             for s in range(K * width // (P * CHUNK)):
@@ -412,10 +431,11 @@ def tile_chainlveg_pb_k_kernel(
 
         load(0)
         load(1)
-        load_child()
-        for n in range(2, AHEAD):
-            load(n)
         load_small()
+        load(2)
+        load_child()
+        for n in range(3, AHEAD):
+            load(n)
         x_grouped = {}
 
         def regroup(n):
@@ -434,15 +454,15 @@ def tile_chainlveg_pb_k_kernel(
                 var_child_high_parts()
             if n == 4:
                 var_child_low_parts()
-            if n == 5:
-                turn_masks()
-                child_weights()
-            if n == var_done - 2:
+            if n + AHEAD == var_done - 1:
                 load_biases()
             quantise_x(n, x_grouped[n])
             quantise_weights(n)
             if n >= 1:
                 multiply(n - 1)
+            if n == 1:
+                turn_masks()
+                child_weights()
         sv, ss, q, mx = regroup_on_vector, regroup_on_scalar, quantise_weights, multiply
 
         def prefetch(n):
@@ -469,68 +489,76 @@ def tile_chainlveg_pb_k_kernel(
         sv(n)
         ss(n)
         prefetch(n + 1)
+        first_half("var")
         sv(n + 1)
         ss(n + 1)
-        first_half("var")
-        q(n)
         second_half("var")
-        mx(n)
-        for r in range(4):
-            inverse_root(r)
+        q(n)
+        for r in range(CHUNKS):
+            log_of_sum(r)
+            if r == 0:
+                mx(n)
             prefetch(n + 2 + r)
             sv(n + 2 + r)
             ss(n + 2 + r)
             q(n + 1 + r)
             mx(n + 1 + r)
         n = n + 6
-        product_of_roots(0)
-        prefetch(n)
-        sv(n)
-        ss(n)
+        for r in range(2):
+            prefetch(n + r)
+            inverse_root(r)
+            q(n - 1 + r)
+            mx(n - 1 + r)
+            sv(n + r)
+            ss(n + 2 + r)
+        n = n + 2
         q(n - 1)
         mx(n - 1)
-        log_of_product(0)
-        n = n + 1
-        prefetch(n)
         sv(n)
-        ss(n)
-        product_of_roots(1)
-        q(n - 1)
-        mx(n - 1)
-        n = n + 1
-        prefetch(n)
-        sv(n)
-        log_of_product(1)
-        q(n - 1)
-        mx(n - 1)
-        log_terms(0)
         first_half("mean")
-        ss(n)
         second_half("mean")
-        sv(n + 1)
-        log_terms(1)
-        ss(n + 1)
+        inverse_root(2)
         q(n)
-        differences(0)
-        differences(1)
-        sv(n + 2)
+        sv(n + 1)
+        weighed_difference(0)
+        square_difference(0)
+        weighed_difference(1)
+        square_difference(1)
         ss(n + 2)
         mx(n)
         q(n + 1)
+        inverse_root(3)
+        weighed_difference(2)
+        square_difference(2)
+        for b in range(B):
+            add_child_term(0, b)
         mx(n + 1)
-        add_square(0)
-        sv(n + 3)
+        sv(n + 2)
         ss(n + 3)
-        differences(2)
-        differences(3)
+        weighed_difference(3)
+        square_difference(3)
         q(n + 2)
+        for b in range(B):
+            add_child_term(1, b)
         mx(n + 2)
-        add_square(1)
+        sv(n + 3)
         q(n + 3)
+        for b in range(B):
+            add_child_term(2, b)
         mx(n + 3)
-        add_square(2)
         for b in range(B):
             transition_weight(b, acc["weight"][b])
-        add_transition_weight(0)
-        add_square(3)
-        add_transition_weight(1)
+        for b in range(B):
+            rows = child_term[b].rearrange("p (i m) -> p i m", i=NL)[:, NL - NI :]
+            nc.vector.tensor_tensor(
+                out=rows,
+                in0=rows,
+                in1=tw_terms[b].rearrange("p n t u -> p (n t u)").unsqueeze(1).to_broadcast([P, NI, NL * NL * T * T]),
+                op=ALU.add,
+            )
+        for b in range(B):
+            add_child_term(CHUNKS - 1, b)
+            store(CHUNKS - 1, b)
+        for ic in range(CHUNKS - 1):
+            for b in range(B):
+                add_transition_weight(ic, b)

@@ -68,13 +68,13 @@ def tile_chainlveg_pb_k_kernel(
         weight1 = const.tile([P, B, W_WEIGHT], BF16, name="weight1")
 
         def load_child():
-            nc.sync.dma_start(out=log_std1, in_=cs_var.rearrange("b p i j t e g -> p b (i j t e g)"))
-            nc.sync.dma_start(out=mean1, in_=cs_mu.rearrange("b p i j t e g -> p b (i j t e g)"))
+            nc.scalar.dma_start(out=log_std1, in_=cs_var.rearrange("b p i j t e g -> p b (i j t e g)"))
+            nc.scalar.dma_start(out=mean1, in_=cs_mu.rearrange("b p i j t e g -> p b (i j t e g)"))
 
         def load_small():
-            nc.sync.dma_start(out=weight1, in_=cs_scale.rearrange("b p i j t e -> p b (i j t e)"))
-            nc.sync.dma_start(out=mask_rows[0:B, :], in_=mask_here)
-            nc.sync.dma_start(out=mask_rows[B : 2 * B, :], in_=mask_next)
+            nc.scalar.dma_start(out=weight1, in_=cs_scale.rearrange("b p i j t e -> p b (i j t e)"))
+            nc.scalar.dma_start(out=mask_rows[0:B, :], in_=mask_here)
+            nc.scalar.dma_start(out=mask_rows[B : 2 * B, :], in_=mask_next)
 
         mask_rows = const.tile([P, P], BF16, name="mask_rows")
         nc.vector.memset(mask_rows, 0.0)
@@ -249,20 +249,25 @@ def tile_chainlveg_pb_k_kernel(
 
         codes = {}
 
-        def quantise_weights(n):
-            codes[n] = (
-                w_mx.tile([P, CHUNK // PACK], U32, name="w_codes", align_bytes=64),
-                w_mx.tile([P, CHUNK // PACK], U8, name="w_scales", align_bytes=64),
+        def quantise_weights(n, part=0, parts_of=1):
+            if part == 0:
+                codes[n] = (
+                    w_mx.tile([P, CHUNK // PACK], U32, name="w_codes", align_bytes=64),
+                    w_mx.tile([P, CHUNK // PACK], U8, name="w_scales", align_bytes=64),
+                )
+            cols = slice(part * CHUNK // parts_of, (part + 1) * CHUNK // parts_of)
+            words = slice(part * CHUNK // parts_of // PACK, (part + 1) * CHUNK // parts_of // PACK)
+            nc.vector.quantize_mx(
+                out=codes[n][0][:, words].bitcast(FP8X4), scales=codes[n][1][:, words], in_=grouped[n][:, cols]
             )
-            nc.vector.quantize_mx(out=codes[n][0].bitcast(FP8X4), scales=codes[n][1], in_=grouped[n])
 
-        def multiply(n):
+        def multiply(n, part=0, parts_of=1):
             key, w, width, vector_passes, s = pieces[n]
             passes = CHUNK // (PACK * width)
-            if s == 0:
+            if s == 0 and part == 0:
                 acc[key] = [psum_acc.tile([P, width], F32, name="acc", tag="acc%d" % b) for b in range(B)]
             w_codes, w_scales = codes[n]
-            for c in range(passes):
+            for c in range(part * passes // parts_of, (part + 1) * passes // parts_of):
                 k_pass = s * passes + c
                 w_cols = slice(c * width, (c + 1) * width)
                 for b in range(B):
@@ -430,11 +435,9 @@ def tile_chainlveg_pb_k_kernel(
                 load_weights(n, w, width, s, part, parts_of)
 
         load(0)
-        load(1)
         load_small()
-        load(2)
         load_child()
-        for n in range(3, AHEAD):
+        for n in range(1, AHEAD):
             load(n)
         x_grouped = {}
 
@@ -457,9 +460,16 @@ def tile_chainlveg_pb_k_kernel(
             if n + AHEAD == var_done - 1:
                 load_biases()
             quantise_x(n, x_grouped[n])
-            quantise_weights(n)
-            if n >= 1:
+            if n >= 1 and n == var_done - 1:
                 multiply(n - 1)
+            if n == var_done - 1:
+                for part in range(2):
+                    quantise_weights(n, part, 2)
+                    multiply(n, part, 2)
+            else:
+                quantise_weights(n)
+                if n >= 1:
+                    multiply(n - 1)
             if n == 1:
                 turn_masks()
                 child_weights()
@@ -485,7 +495,6 @@ def tile_chainlveg_pb_k_kernel(
 
         n = var_done
         prefetch(n)
-        mx(n - 1)
         sv(n)
         ss(n)
         prefetch(n + 1)
@@ -512,8 +521,9 @@ def tile_chainlveg_pb_k_kernel(
             sv(n + r)
             ss(n + 2 + r)
         n = n + 2
-        q(n - 1)
-        mx(n - 1)
+        for part in range(2):
+            q(n - 1, part, 2)
+            mx(n - 1, part, 2)
         sv(n)
         first_half("mean")
         second_half("mean")
@@ -542,10 +552,12 @@ def tile_chainlveg_pb_k_kernel(
             add_child_term(1, b)
         mx(n + 2)
         sv(n + 3)
-        q(n + 3)
+        for part in range(2):
+            q(n + 3, part, 2)
         for b in range(B):
             add_child_term(2, b)
-        mx(n + 3)
+        for part in range(2):
+            mx(n + 3, part, 2)
         for b in range(B):
             transition_weight(b, acc["weight"][b])
         for b in range(B):

@@ -185,7 +185,7 @@ def tile_chainlveg_pb_k_kernel(
         x_codes = const.tile([P, K // K_PASS * B * P], U32, name="x_codes", align_bytes=64)
         x_scales = const.tile([P, K // K_PASS * B * P], U8, name="x_scales", align_bytes=64)
 
-        x_raws, w_raws = {}, {}
+        x_raws, w_raws, x_grouped = {}, {}, {}
         acc, grouped, pieces = {}, {}, []
 
         def load_x(n, part, parts_of):
@@ -198,22 +198,26 @@ def tile_chainlveg_pb_k_kernel(
                 in_=x_next[:, :, n * cols : (n + 1) * cols].rearrange("b r k -> r b k")[:, :, k],
             )
 
-        def transpose_x(n):
+        def transpose_x(n, part=0, parts_of=1):
             x_raw = x_raws[n]
             words = x_raw.bitcast(F32).rearrange("r (b c p u) -> r b c u p", b=B, c=X_PASSES, u=2)
-            x_grouped = big.tile([P, CHUNK], BF16, name="x_grouped", tag="big", align_bytes=64)
-            grouped_words = x_grouped.bitcast(F32).rearrange("p (c b r u) -> p c b r u", c=X_PASSES, b=B, u=2)
-            for c in range(X_PASSES):
+            if part == 0:
+                x_grouped[n] = big.tile([P, CHUNK], BF16, name="x_grouped", tag="big", align_bytes=64)
+            grouped_words = x_grouped[n].bitcast(F32).rearrange("p (c b r u) -> p c b r u", c=X_PASSES, b=B, u=2)
+            for c in range(part * X_PASSES // parts_of, (part + 1) * X_PASSES // parts_of):
                 xt = psum_t.tile([P, B, 2, P], F32, name="xt", tag="xt")
                 for b in range(B):
                     for u in range(2):
                         nc.tensor.transpose(out=xt[:, b, u, :], in_=words[:, b, c, u, :], identity=ident_f)
                 nc.scalar.copy(out=grouped_words[:, c], in_=xt.rearrange("p b u r -> p b r u"))
-            return x_grouped
 
-        def quantise_x(n, x_grouped):
-            cols = slice(n * CHUNK // PACK, (n + 1) * CHUNK // PACK)
-            nc.vector.quantize_mx(out=x_codes[:, cols].bitcast(FP8X4), scales=x_scales[:, cols], in_=x_grouped)
+        def quantise_x(n, part=0, parts_of=1):
+            size = CHUNK // parts_of
+            values = slice(part * size, (part + 1) * size)
+            cols = slice((n * CHUNK + part * size) // PACK, (n * CHUNK + (part + 1) * size) // PACK)
+            nc.vector.quantize_mx(
+                out=x_codes[:, cols].bitcast(FP8X4), scales=x_scales[:, cols], in_=x_grouped[n][:, values]
+            )
 
         def load_weights(n, w, width, s, part, parts_of):
             passes = CHUNK // (PACK * width)
@@ -412,8 +416,8 @@ def tile_chainlveg_pb_k_kernel(
 
         streams = (
             ("var", tpv_w, W_GAUSS, (2, 3)),
-            ("mean", tpm_w, W_GAUSS, (0, 2, 4, 4, 4, 4, 4, 4)),
-            ("weight", tw_w, W_WEIGHT, (2, 4, 6, 6)),
+            ("mean", tpm_w, W_GAUSS, (2, 2, 4, 4, 4, 4, 4, 4)),
+            ("weight", tw_w, W_WEIGHT, (2, 4, 4, 6)),
         )
         for key, w, width, vector_passes in streams:
             for s in range(K * width // (P * CHUNK)):
@@ -429,6 +433,11 @@ def tile_chainlveg_pb_k_kernel(
                 return
             key, w, width, vector_passes, s = pieces[n]
             parts_of = LOAD_PARTS.get(n, 1)
+            if n == X_CHUNKS - 1:
+                load_x(n, 0, 2)
+                load_weights(n, w, width, s, 0, 1)
+                load_x(n, 1, 2)
+                return
             for part in range(parts_of):
                 if n < X_CHUNKS:
                     load_x(n, part, parts_of)
@@ -439,16 +448,14 @@ def tile_chainlveg_pb_k_kernel(
         load_child()
         for n in range(1, AHEAD):
             load(n)
-        x_grouped = {}
-
         def regroup(n):
             load(n + AHEAD)
             if n <= last:
                 regroup_on_vector(n)
                 regroup_on_scalar(n)
 
-        for n in range(X_CHUNKS):
-            x_grouped[n] = transpose_x(n)
+        for n in range(X_CHUNKS - 1):
+            transpose_x(n)
             regroup(n)
             if n == 2:
                 nc.scalar.activation(out=var1, in_=log_std1, func=ACT.Exp, scale=2.0)
@@ -459,20 +466,23 @@ def tile_chainlveg_pb_k_kernel(
                 var_child_low_parts()
             if n + AHEAD == var_done - 1:
                 load_biases()
-            quantise_x(n, x_grouped[n])
-            if n >= 1 and n == var_done - 1:
+            quantise_x(n)
+            quantise_weights(n)
+            if n >= 1:
                 multiply(n - 1)
-            if n == var_done - 1:
-                for part in range(2):
-                    quantise_weights(n, part, 2)
-                    multiply(n, part, 2)
-            else:
-                quantise_weights(n)
-                if n >= 1:
-                    multiply(n - 1)
             if n == 1:
                 turn_masks()
                 child_weights()
+        n = X_CHUNKS - 1
+        transpose_x(n, 0, 2)
+        regroup(n)
+        multiply(n - 1)
+        transpose_x(n, 1, 2)
+        quantise_x(n, 0, 2)
+        quantise_weights(n)
+        multiply(n, 0, 2)
+        quantise_x(n, 1, 2)
+        multiply(n, 1, 2)
         sv, ss, q, mx = regroup_on_vector, regroup_on_scalar, quantise_weights, multiply
 
         def prefetch(n):
@@ -525,52 +535,49 @@ def tile_chainlveg_pb_k_kernel(
             q(n - 1, part, 2)
             mx(n - 1, part, 2)
         sv(n)
+        q(n)
+        mx(n)
         first_half("mean")
         second_half("mean")
+        ss(n + 2)
         inverse_root(2)
-        q(n)
         sv(n + 1)
+        q(n + 1)
         weighed_difference(0)
         square_difference(0)
         weighed_difference(1)
         square_difference(1)
-        ss(n + 2)
-        mx(n)
-        q(n + 1)
+        mx(n + 1)
         inverse_root(3)
+        sv(n + 2)
         weighed_difference(2)
         square_difference(2)
-        for b in range(B):
-            add_child_term(0, b)
-        mx(n + 1)
-        sv(n + 2)
-        ss(n + 3)
-        weighed_difference(3)
-        square_difference(3)
         q(n + 2)
         for b in range(B):
-            add_child_term(1, b)
-        mx(n + 2)
+            add_child_term(0, b)
+        ss(n + 3)
         sv(n + 3)
-        for part in range(2):
-            q(n + 3, part, 2)
+        mx(n + 2)
+        weighed_difference(3)
+        square_difference(3)
+        q(n + 3)
         for b in range(B):
-            add_child_term(2, b)
-        for part in range(2):
-            mx(n + 3, part, 2)
+            add_child_term(1, b)
+        mx(n + 3)
         for b in range(B):
             transition_weight(b, acc["weight"][b])
         for b in range(B):
-            rows = child_term[b].rearrange("p (i m) -> p i m", i=NL)[:, NL - NI :]
+            rows = child_term[b].rearrange("p (i m) -> p i m", i=NL)[:, NL - 2 * NI :]
             nc.vector.tensor_tensor(
                 out=rows,
                 in0=rows,
-                in1=tw_terms[b].rearrange("p n t u -> p (n t u)").unsqueeze(1).to_broadcast([P, NI, NL * NL * T * T]),
+                in1=tw_terms[b].rearrange("p n t u -> p (n t u)").unsqueeze(1).to_broadcast([P, 2 * NI, NL * NL * T * T]),
                 op=ALU.add,
             )
-        for b in range(B):
-            add_child_term(CHUNKS - 1, b)
-            store(CHUNKS - 1, b)
-        for ic in range(CHUNKS - 1):
+        for ic in range(CHUNKS - 2):
             for b in range(B):
                 add_transition_weight(ic, b)
+        for ic in range(CHUNKS - 2, CHUNKS):
+            for b in range(B):
+                add_child_term(ic, b)
+                store(ic, b)

@@ -86,6 +86,8 @@ def tile_chainlveg_pb_k_kernel(
             mask_cols = psum_t.tile([P, P], BF16, name="mask_cols", tag="xt")
             nc.tensor.transpose(out=mask_cols, in_=mask_rows, identity=ident_b)
             nc.vector.tensor_copy(out=factors, in_=mask_cols[:, 0 : 2 * B])
+
+        def mask_products():
             nc.vector.tensor_tensor(out=both, in0=factors[:, 0:B], in1=factors[:, B : 2 * B], op=ALU.mult)
             nc.vector.tensor_scalar(out=minus_half, in0=both, scalar1=-0.5, scalar2=None, op0=ALU.mult)
 
@@ -105,13 +107,15 @@ def tile_chainlveg_pb_k_kernel(
                     scalar2=None,
                     op0=ALU.mult,
                 )
-                nc.vector.tensor_copy(
-                    out=child_term[b].rearrange("p (n k c) -> p n k c", n=NL * NL, k=NL),
-                    in_=weight1_here[:, b]
-                    .rearrange("p n t u -> p n (t u)")
-                    .unsqueeze(2)
-                    .to_broadcast([P, NL * NL, NL, T * T]),
-                )
+
+        def expand_child_weights(b, copy):
+            copy(
+                out=child_term[b].rearrange("p (n k c) -> p n k c", n=NL * NL, k=NL),
+                in_=weight1_here[:, b]
+                .rearrange("p n t u -> p n (t u)")
+                .unsqueeze(2)
+                .to_broadcast([P, NL * NL, NL, T * T]),
+            )
 
         ones_c = const.tile([P, PART], BF16, name="ones_c")
         nc.vector.tensor_tensor(out=ones_c, in0=ident_b[:, 0:PART], in1=ident_b[:, PART : 2 * PART], op=ALU.add)
@@ -156,9 +160,10 @@ def tile_chainlveg_pb_k_kernel(
         var1 = const.tile([P, B, W_GAUSS], F32, name="var1")
         child_sets = [(b, g) for b in range(B) for g in range(G)]
 
+        for b in range(B):
+            nc.vector.memset(parts["mean", b][:, :, 1, :], 0.0)
+
         def mean_child_parts():
-            for b in range(B):
-                nc.vector.memset(parts["mean", b][:, :, 1, :], 0.0)
             for b, g in child_sets:
                 nc.vector.tensor_copy(out=part_view("mean", b, g, 0), in_=child_view(mean1[:, b], g))
 
@@ -175,12 +180,44 @@ def tile_chainlveg_pb_k_kernel(
                     op=ALU.subtract,
                 )
 
+        bias_rows = const.tile([P, P], BF16, name="bias_rows")
+        nc.vector.memset(bias_rows, 0.0)
+        biases = (("var", tpv_b, W_GAUSS), ("mean", tpm_b, W_GAUSS), ("weight", tw_b, W_WEIGHT))
+        BIAS_ROWS = sum(width // P for key, vector, width in biases)
         bias = {}
 
         def load_biases():
-            for key, vector, width in (("var", tpv_b, W_GAUSS), ("mean", tpm_b, W_GAUSS), ("weight", tw_b, W_WEIGHT)):
-                bias[key] = const.tile([P, width], BF16, name="bias_" + key)
-                nc.sync.dma_start(out=bias[key], in_=vector.partition_broadcast(P))
+            row = 0
+            for key, vector, width in biases:
+                rows = width // P
+                nc.sync.dma_start(out=bias_rows[row : row + rows, :], in_=vector.rearrange("(r c) -> r c", c=P))
+                row += rows
+
+        bias_cols = const.tile([P, BIAS_ROWS], BF16, name="bias_cols")
+        spread_all = const.tile([P, BIAS_ROWS, P], BF16, name="bias")
+        bias_psum = {}
+
+        def turn_bias_rows():
+            bias_psum["rows"] = psum_acc.tile([P, P], BF16, name="turned_rows", tag="acc0")
+            nc.tensor.transpose(out=bias_psum["rows"], in_=bias_rows, identity=ident_b)
+
+        def take_bias_cols():
+            nc.vector.tensor_copy(out=bias_cols, in_=bias_psum["rows"][:, 0:BIAS_ROWS])
+
+        def turn_bias_cols():
+            bias_psum["all"] = psum_acc.tile([P, BIAS_ROWS, P], BF16, name="bias_psum", tag="acc1")
+            for r in range(BIAS_ROWS):
+                nc.tensor.transpose(
+                    out=bias_psum["all"][:, r, :], in_=bias_cols[:, r : r + 1].to_broadcast([P, P]), identity=ident_b
+                )
+
+        def take_biases():
+            nc.vector.tensor_copy(out=spread_all, in_=bias_psum["all"])
+            row = 0
+            for key, vector, width in biases:
+                rows = width // P
+                bias[key] = spread_all[:, row : row + rows, :].rearrange("p r c -> p (r c)")
+                row += rows
 
         x_codes = const.tile([P, K // K_PASS * B * P], U32, name="x_codes", align_bytes=64)
         x_scales = const.tile([P, K // K_PASS * B * P], U8, name="x_scales", align_bytes=64)
@@ -241,9 +278,11 @@ def tile_chainlveg_pb_k_kernel(
         def regroup_on_vector(n):
             key, w, width, vector_passes, s = pieces[n]
             src, dst, passes = regroup_views(n, width)
-            for c in range(0, vector_passes, 2):
-                pair = slice(c, min(c + 2, vector_passes))
-                nc.vector.tensor_copy(out=dst[:, pair], in_=src[:, pair])
+            even = vector_passes - vector_passes % 2
+            if even:
+                nc.vector.tensor_copy(out=dst[:, :even], in_=src[:, :even])
+            if even < vector_passes:
+                nc.vector.tensor_copy(out=dst[:, even], in_=src[:, even])
 
         def regroup_on_scalar(n):
             key, w, width, vector_passes, s = pieces[n]
@@ -296,12 +335,15 @@ def tile_chainlveg_pb_k_kernel(
 
         turned = {}
 
-        def split_parent(key, b, term):
-            values = term[:, b].rearrange("p (q w g) -> p g q w", q=JGROUPS, g=G)
-            high = parts[key, b][:, :, 2, :].rearrange("p (g q) w -> p g q w", g=G)
-            low = parts[key, b][:, :, 3, :].rearrange("p (g q) w -> p g q w", g=G)
-            nc.vector.tensor_copy(out=high, in_=values)
-            nc.vector.tensor_tensor(out=low, in0=values, in1=high, op=ALU.subtract)
+        def split_parents(key):
+            def part(b, which):
+                return parts[key, b][:, :, which, :].rearrange("p (g q) w -> p g q w", g=G)
+
+            values = [parent[key][:, b].rearrange("p (q w g) -> p g q w", q=JGROUPS, g=G) for b in range(B)]
+            for b in range(B):
+                nc.vector.tensor_copy(out=part(b, 2), in_=values[b])
+            for b in range(B):
+                nc.vector.tensor_tensor(out=part(b, 3), in0=values[b], in1=part(b, 2), op=ALU.subtract)
 
         def turn_parts(key, b):
             if key not in turned:
@@ -313,7 +355,12 @@ def tile_chainlveg_pb_k_kernel(
                     in_=parts[key, b][:, q].rearrange("p a w -> p (a w)"),
                     identity=ident_b,
                 )
-            nc.scalar.copy(out=turned[key][:, :, b, :], in_=in_psum)
+            turned_psum[key, b] = in_psum
+
+        turned_psum = {}
+
+        def take_parts(key, b, copy):
+            copy(out=turned[key][:, :, b, :], in_=turned_psum[key, b])
 
         def pair_sums(key, ic, g, h):
             sums = psum_t.tile([P, 2, B * P], F32, name="sums", tag="xt")
@@ -384,19 +431,21 @@ def tile_chainlveg_pb_k_kernel(
 
         tw_terms = {}
 
-        def transition_weight(b, acc):
-            tw = const.tile([P, W_WEIGHT], F32, name="tw%d" % b)
-            nc.vector.tensor_tensor(out=tw, in0=acc, in1=bias["weight"], op=ALU.add)
-            tw_t = const.tile([P, NL * NL, T, T], F32, name="tw_t%d" % b)
-            nc.vector.tensor_scalar(
-                out=tw_t,
-                in0=tw.rearrange("p (n u) -> p n u", u=T).unsqueeze(2).to_broadcast([P, NL * NL, T, T]),
-                scalar1=-LOG_2PI,
-                scalar2=both[:, b : b + 1],
-                op0=ALU.add,
-                op1=ALU.mult,
-            )
-            tw_terms[b] = tw_t
+        def transition_weights():
+            tw = []
+            for b in range(B):
+                tw.append(const.tile([P, W_WEIGHT], F32, name="tw%d" % b))
+                nc.vector.tensor_tensor(out=tw[b], in0=acc["weight"][b], in1=bias["weight"], op=ALU.add)
+            for b in range(B):
+                tw_terms[b] = const.tile([P, NL * NL, T, T], F32, name="tw_t%d" % b)
+                nc.vector.tensor_scalar(
+                    out=tw_terms[b],
+                    in0=tw[b].rearrange("p (n u) -> p n u", u=T).unsqueeze(2).to_broadcast([P, NL * NL, T, T]),
+                    scalar1=-LOG_2PI,
+                    scalar2=both[:, b : b + 1],
+                    op0=ALU.add,
+                    op1=ALU.mult,
+                )
 
         def add_transition_weight(ic, b):
             rows = result[b].rearrange("p (i m) -> p i m", i=NL)[:, ic * NI : (ic + 1) * NI]
@@ -415,9 +464,9 @@ def tile_chainlveg_pb_k_kernel(
             )
 
         streams = (
-            ("var", tpv_w, W_GAUSS, (2, 3)),
+            ("var", tpv_w, W_GAUSS, (3,)),
             ("mean", tpm_w, W_GAUSS, (2, 2, 4, 4, 4, 4, 4, 4)),
-            ("weight", tw_w, W_WEIGHT, (2, 4, 4, 6)),
+            ("weight", tw_w, W_WEIGHT, (2, 4, 4, 4)),
         )
         for key, w, width, vector_passes in streams:
             for s in range(K * width // (P * CHUNK)):
@@ -433,14 +482,10 @@ def tile_chainlveg_pb_k_kernel(
                 return
             key, w, width, vector_passes, s = pieces[n]
             parts_of = LOAD_PARTS.get(n, 1)
-            if n == X_CHUNKS - 1:
-                load_x(n, 0, 2)
-                load_weights(n, w, width, s, 0, 1)
-                load_x(n, 1, 2)
-                return
-            for part in range(parts_of):
-                if n < X_CHUNKS:
+            if n < X_CHUNKS:
+                for part in range(parts_of):
                     load_x(n, part, parts_of)
+            for part in range(parts_of):
                 load_weights(n, w, width, s, part, parts_of)
 
         load(0)
@@ -459,30 +504,39 @@ def tile_chainlveg_pb_k_kernel(
             regroup(n)
             if n == 2:
                 nc.scalar.activation(out=var1, in_=log_std1, func=ACT.Exp, scale=2.0)
-                mean_child_parts()
+            if n == 4:
+                expand_child_weights(0, nc.scalar.copy)
             if n == 3:
                 var_child_high_parts()
             if n == 4:
                 var_child_low_parts()
-            if n + AHEAD == var_done - 1:
+            if n == 0:
                 load_biases()
+            if n == 4:
+                turn_bias_rows()
+            if n == 5:
+                take_bias_cols()
+            if n == 6:
+                turn_bias_cols()
             quantise_x(n)
             quantise_weights(n)
             if n >= 1:
                 multiply(n - 1)
             if n == 1:
                 turn_masks()
+                mean_child_parts()
                 child_weights()
+                mask_products()
+                expand_child_weights(1, nc.vector.tensor_copy)
         n = X_CHUNKS - 1
-        transpose_x(n, 0, 2)
+        take_biases()
+        transpose_x(n)
         regroup(n)
+        quantise_x(n)
         multiply(n - 1)
-        transpose_x(n, 1, 2)
-        quantise_x(n, 0, 2)
-        quantise_weights(n)
-        multiply(n, 0, 2)
-        quantise_x(n, 1, 2)
-        multiply(n, 1, 2)
+        for part in range(2):
+            quantise_weights(n, part, 2)
+            multiply(n, part, 2)
         sv, ss, q, mx = regroup_on_vector, regroup_on_scalar, quantise_weights, multiply
 
         def prefetch(n):
@@ -494,10 +548,12 @@ def tile_chainlveg_pb_k_kernel(
                 nc.scalar.activation(out=parent[key], in_=parent[key], func=ACT.Exp, scale=2.0)
 
         def second_half(key):
-            for b in range(B):
-                split_parent(key, b, parent[key])
+            split_parents(key)
             for b in range(B):
                 turn_parts(key, b)
+            take_parts(key, 0, nc.scalar.copy)
+            if key == "var":
+                take_parts(key, 1, nc.scalar.copy)
 
         def differences(m):
             weighed_difference(m)
@@ -539,9 +595,10 @@ def tile_chainlveg_pb_k_kernel(
         mx(n)
         first_half("mean")
         second_half("mean")
+        sv(n + 1)
+        take_parts("mean", 1, nc.vector.tensor_copy)
         ss(n + 2)
         inverse_root(2)
-        sv(n + 1)
         q(n + 1)
         weighed_difference(0)
         square_difference(0)
@@ -564,8 +621,7 @@ def tile_chainlveg_pb_k_kernel(
         for b in range(B):
             add_child_term(1, b)
         mx(n + 3)
-        for b in range(B):
-            transition_weight(b, acc["weight"][b])
+        transition_weights()
         for b in range(B):
             rows = child_term[b].rearrange("p (i m) -> p i m", i=NL)[:, NL - 2 * NI :]
             nc.vector.tensor_tensor(

import math
from contextlib import ExitStack

import concourse.mybir as mybir
from concourse.masks import make_identity

FP8X4 = mybir.dt.float8_e4m3fn_x4
BF16 = mybir.dt.bfloat16
F32 = mybir.dt.float32
U32 = mybir.dt.uint32
U8 = mybir.dt.uint8
ALU = mybir.AluOpType
ACT = mybir.ActivationFunctionType

P = 128
B = 2
K = 16384
NL, T, G = 8, 2, 2
KU = NL * T
W_WEIGHT = NL * NL * T
W_GAUSS = W_WEIGHT * G
CLIP = 1.0
LOG_2PI = math.log(2.0 * math.pi)

JG = 2
JGROUPS = NL // JG
PART = NL * JG * T
GROUPS = G * JGROUPS
NI = 2
CHUNKS = NL // NI
M = NI * JG * NL * T * T
N_OUT = NL * NL * NL * T * T
BIG = 16
RUN = 8
LOAD_PARTS = {0: 2, 1: 2}
AHEAD = 4
HALVES = 2
GCOLS = NL * JG * NL * T * T

PACK = 4
K_PASS = P * PACK
CHUNK = 4096
X_PASSES = CHUNK // (PACK * B * P)
X_CHUNKS = K // (X_PASSES * K_PASS)

FLOPS = 2 * B * P * K * (W_WEIGHT + 2 * W_GAUSS)


def tile_chainlveg_pb_k_kernel(
    tc, x_next, cs_scale, cs_mu, cs_var, mask_here, mask_next, tw_w, tw_b, tpm_w, tpm_b, tpv_w, tpv_b, out
):
    nc = tc.nc
    with ExitStack() as stack:
        stack.enter_context(tc.manual_schedule())
        const = stack.enter_context(tc.tile_pool(name="const", bufs=1))
        big = stack.enter_context(tc.tile_pool(name="big", bufs=BIG))
        w_mx = stack.enter_context(tc.tile_pool(name="w_mx", bufs=3))
        psum_t = stack.enter_context(tc.psum_pool(name="psum_t", bufs=4))
        psum_acc = stack.enter_context(tc.psum_pool(name="psum_acc", bufs=2))

        ident_f = const.tile([P, P], F32, name="ident_f")
        make_identity(nc, ident_f)
        ident_b = const.tile([P, P], BF16, name="ident_b")
        make_identity(nc, ident_b)

        mean1 = const.tile([P, B, W_GAUSS], BF16, name="mean1")
        log_std1 = const.tile([P, B, W_GAUSS], BF16, name="log_std1")
        weight1 = const.tile([P, B, W_WEIGHT], BF16, name="weight1")

        def load_child():
            nc.scalar.dma_start(out=log_std1, in_=cs_var.rearrange("b p i j t e g -> p b (i j t e g)"))
            nc.scalar.dma_start(out=mean1, in_=cs_mu.rearrange("b p i j t e g -> p b (i j t e g)"))

        def load_small():
            nc.scalar.dma_start(out=weight1, in_=cs_scale.rearrange("b p i j t e -> p b (i j t e)"))
            nc.scalar.dma_start(out=mask_rows[0:B, :], in_=mask_here)
            nc.scalar.dma_start(out=mask_rows[B : 2 * B, :], in_=mask_next)

        mask_rows = const.tile([P, P], BF16, name="mask_rows")
        nc.vector.memset(mask_rows, 0.0)
        factors = const.tile([P, 2 * B], F32, name="factors")
        both = const.tile([P, B], F32, name="both")
        minus_half = const.tile([P, B], F32, name="minus_half")

        def turn_masks():
            mask_cols = psum_t.tile([P, P], BF16, name="mask_cols", tag="xt")
            nc.tensor.transpose(out=mask_cols, in_=mask_rows, identity=ident_b)
            nc.vector.tensor_copy(out=factors, in_=mask_cols[:, 0 : 2 * B])

        def mask_products():
            nc.vector.tensor_tensor(out=both, in0=factors[:, 0:B], in1=factors[:, B : 2 * B], op=ALU.mult)
            nc.vector.tensor_scalar(out=minus_half, in0=both, scalar1=-0.5, scalar2=None, op0=ALU.mult)

        weight1_here = const.tile([P, B, NL * NL, T, T], F32, name="weight1_here")

        child_term = [const.tile([P, N_OUT], F32, name="child_term%d" % b) for b in range(B)]

        def child_weights():
            for b in range(B):
                nc.vector.tensor_scalar(
                    out=weight1_here[:, b],
                    in0=weight1[:, b]
                    .rearrange("p (n t) -> p n t", t=T)
                    .unsqueeze(3)
                    .to_broadcast([P, NL * NL, T, T]),
                    scalar1=factors[:, b : b + 1],
                    scalar2=None,
                    op0=ALU.mult,
                )

        def expand_child_weights(b, copy):
            copy(
                out=child_term[b].rearrange("p (n k c) -> p n k c", n=NL * NL, k=NL),
                in_=weight1_here[:, b]
                .rearrange("p n t u -> p n (t u)")
                .unsqueeze(2)
                .to_broadcast([P, NL * NL, NL, T * T]),
            )

        ones_c = const.tile([P, PART], BF16, name="ones_c")
        nc.vector.tensor_tensor(out=ones_c, in0=ident_b[:, 0:PART], in1=ident_b[:, PART : 2 * PART], op=ALU.add)
        ones_q = const.tile([P, PART], BF16, name="ones_q")
        nc.vector.tensor_tensor(
            out=ones_q, in0=ident_b[:, 2 * PART : 3 * PART], in1=ident_b[:, 3 * PART : 4 * PART], op=ALU.add
        )
        spread = {}
        for key, sign in (("var", 1.0), ("mean", -1.0)):
            spread[key] = const.tile([P, GCOLS], BF16, name="spread_" + key)
            for t in range(T):
                nc.vector.tensor_copy(
                    out=spread[key].rearrange("p (a k t u) -> p t a k u", a=NL * JG, k=NL, t=T)[:, t],
                    in_=ones_c.rearrange("p (a t) -> p t a", t=T)[:, t]
                    .unsqueeze(2)
                    .unsqueeze(3)
                    .to_broadcast([P, NL * JG, NL, T]),
                )
            for t in range(T):
                cols_t = spread[key].rearrange("p (i c t u) -> p t i c u", i=NL, t=T, u=T)[:, t]
                nc.vector.scalar_tensor_tensor(
                    out=cols_t,
                    in0=ones_q.rearrange("p (c u) -> p c u", u=T).unsqueeze(1).to_broadcast([P, NL, JG * NL, T]),
                    scalar=sign,
                    in1=cols_t,
                    op0=ALU.mult,
                    op1=ALU.add,
                )

        parts = {}
        for key in ("var", "mean"):
            for b in range(B):
                parts[key, b] = const.tile([P, GROUPS, 4, PART], BF16, name="parts_%s%d" % (key, b))

        def child_view(values, g):
            return values.rearrange("p (i q m g) -> p g q i m", i=NL, q=JGROUPS, g=G)[:, g]

        def part_view(key, b, g, part):
            ap = parts[key, b][:, g * JGROUPS : (g + 1) * JGROUPS, part, :]
            return ap.rearrange("p q (i m) -> p q i m", i=NL)

        var1 = const.tile([P, B, W_GAUSS], F32, name="var1")
        child_sets = [(b, g) for b in range(B) for g in range(G)]

        for b in range(B):
            nc.vector.memset(parts["mean", b][:, :, 1, :], 0.0)

        def mean_child_parts():
            for b, g in child_sets:
                nc.vector.tensor_copy(out=part_view("mean", b, g, 0), in_=child_view(mean1[:, b], g))

        def var_child_high_parts():
            for b, g in child_sets:
                nc.vector.tensor_copy(out=part_view("var", b, g, 0), in_=child_view(var1[:, b], g))

        def var_child_low_parts():
            for b, g in child_sets:
                nc.vector.tensor_tensor(
                    out=part_view("var", b, g, 1),
                    in0=child_view(var1[:, b], g),
                    in1=part_view("var", b, g, 0),
                    op=ALU.subtract,
                )

        bias_rows = const.tile([P, P], BF16, name="bias_rows")
        nc.vector.memset(bias_rows, 0.0)
        biases = (("var", tpv_b, W_GAUSS), ("mean", tpm_b, W_GAUSS), ("weight", tw_b, W_WEIGHT))
        BIAS_ROWS = sum(width // P for key, vector, width in biases)
        bias = {}

        def load_biases():
            row = 0
            for key, vector, width in biases:
                rows = width // P
                nc.sync.dma_start(out=bias_rows[row : row + rows, :], in_=vector.rearrange("(r c) -> r c", c=P))
                row += rows

        bias_cols = const.tile([P, BIAS_ROWS], BF16, name="bias_cols")
        spread_all = const.tile([P, BIAS_ROWS, P], BF16, name="bias")
        bias_psum = {}

        def turn_bias_rows():
            bias_psum["rows"] = psum_acc.tile([P, P], BF16, name="turned_rows", tag="acc0")
            nc.tensor.transpose(out=bias_psum["rows"], in_=bias_rows, identity=ident_b)

        def take_bias_cols():
            nc.vector.tensor_copy(out=bias_cols, in_=bias_psum["rows"][:, 0:BIAS_ROWS])

        def turn_bias_cols():
            bias_psum["all"] = psum_acc.tile([P, BIAS_ROWS, P], BF16, name="bias_psum", tag="acc1")
            for r in range(BIAS_ROWS):
                nc.tensor.transpose(
                    out=bias_psum["all"][:, r, :], in_=bias_cols[:, r : r + 1].to_broadcast([P, P]), identity=ident_b
                )

        def take_biases():
            nc.vector.tensor_copy(out=spread_all, in_=bias_psum["all"])
            row = 0
            for key, vector, width in biases:
                rows = width // P
                bias[key] = spread_all[:, row : row + rows, :].rearrange("p r c -> p (r c)")
                row += rows

        x_codes = const.tile([P, K // K_PASS * B * P], U32, name="x_codes", align_bytes=64)
        x_scales = const.tile([P, K // K_PASS * B * P], U8, name="x_scales", align_bytes=64)

        x_raws, w_raws, x_grouped = {}, {}, {}
        acc, grouped, pieces = {}, {}, []

        def load_x(n, part, parts_of):
            cols = X_PASSES * K_PASS
            if part == 0:
                x_raws[n] = big.tile([P, B * cols], BF16, name="x_raw", tag="big", align_bytes=64)
            k = slice(part * cols // parts_of, (part + 1) * cols // parts_of)
            nc.sync.dma_start(
                out=x_raws[n].rearrange("r (b k) -> r b k", b=B)[:, :, k],
                in_=x_next[:, :, n * cols : (n + 1) * cols].rearrange("b r k -> r b k")[:, :, k],
            )

        def transpose_x(n, part=0, parts_of=1):
            x_raw = x_raws[n]
            words = x_raw.bitcast(F32).rearrange("r (b c p u) -> r b c u p", b=B, c=X_PASSES, u=2)
            if part == 0:
                x_grouped[n] = big.tile([P, CHUNK], BF16, name="x_grouped", tag="big", align_bytes=64)
            grouped_words = x_grouped[n].bitcast(F32).rearrange("p (c b r u) -> p c b r u", c=X_PASSES, b=B, u=2)
            for c in range(part * X_PASSES // parts_of, (part + 1) * X_PASSES // parts_of):
                xt = psum_t.tile([P, B, 2, P], F32, name="xt", tag="xt")
                for b in range(B):
                    for u in range(2):
                        nc.tensor.transpose(out=xt[:, b, u, :], in_=words[:, b, c, u, :], identity=ident_f)
                nc.scalar.copy(out=grouped_words[:, c], in_=xt.rearrange("p b u r -> p b r u"))

        def quantise_x(n, part=0, parts_of=1):
            size = CHUNK // parts_of
            values = slice(part * size, (part + 1) * size)
            cols = slice((n * CHUNK + part * size) // PACK, (n * CHUNK + (part + 1) * size) // PACK)
            nc.vector.quantize_mx(
                out=x_codes[:, cols].bitcast(FP8X4), scales=x_scales[:, cols], in_=x_grouped[n][:, values]
            )

        def load_weights(n, w, width, s, part, parts_of):
            passes = CHUNK // (PACK * width)
            if part == 0:
                w_raws[n] = big.tile([P, CHUNK], BF16, name="w_raw", tag="big", align_bytes=64)
            rows = w[s * passes * K_PASS : (s + 1) * passes * K_PASS, :]
            c = slice(part * passes // parts_of, (part + 1) * passes // parts_of)
            nc.sync.dma_start(
                out=w_raws[n].rearrange("p (c e) -> p c e", c=passes)[:, c],
                in_=rows.rearrange("(c p j) w -> p c (j w)", c=passes, j=PACK)[:, c],
            )

        def regroup_views(n, width):
            passes = CHUNK // (PACK * width)
            if n not in grouped:
                grouped[n] = big.tile([P, CHUNK], BF16, name="w_grouped", tag="big", align_bytes=64)
            src = w_raws[n].rearrange("p (c j v i) -> p c v j i", c=passes, j=PACK, i=RUN)
            dst = grouped[n].rearrange("p (c v i j) -> p c v j i", c=passes, i=RUN, j=PACK)
            return src, dst, passes

        def regroup_on_vector(n):
            key, w, width, vector_passes, s = pieces[n]
            src, dst, passes = regroup_views(n, width)
            even = vector_passes - vector_passes % 2
            if even:
                nc.vector.tensor_copy(out=dst[:, :even], in_=src[:, :even])
            if even < vector_passes:
                nc.vector.tensor_copy(out=dst[:, even], in_=src[:, even])

        def regroup_on_scalar(n):
            key, w, width, vector_passes, s = pieces[n]
            src, dst, passes = regroup_views(n, width)
            if vector_passes < passes:
                nc.scalar.copy(out=dst[:, vector_passes:], in_=src[:, vector_passes:])

        codes = {}

        def quantise_weights(n, part=0, parts_of=1):
            if part == 0:
                codes[n] = (
                    w_mx.tile([P, CHUNK // PACK], U32, name="w_codes", align_bytes=64),
                    w_mx.tile([P, CHUNK // PACK], U8, name="w_scales", align_bytes=64),
                )
            cols = slice(part * CHUNK // parts_of, (part + 1) * CHUNK // parts_of)
            words = slice(part * CHUNK // parts_of // PACK, (part + 1) * CHUNK // parts_of // PACK)
            nc.vector.quantize_mx(
                out=codes[n][0][:, words].bitcast(FP8X4), scales=codes[n][1][:, words], in_=grouped[n][:, cols]
            )

        def multiply(n, part=0, parts_of=1):
            key, w, width, vector_passes, s = pieces[n]
            passes = CHUNK // (PACK * width)
            if s == 0 and part == 0:
                acc[key] = [psum_acc.tile([P, width], F32, name="acc", tag="acc%d" % b) for b in range(B)]
            w_codes, w_scales = codes[n]
            for c in range(part * passes // parts_of, (part + 1) * passes // parts_of):
                k_pass = s * passes + c
                w_cols = slice(c * width, (c + 1) * width)
                for b in range(B):
                    x_cols = slice((k_pass * B + b) * P, (k_pass * B + b + 1) * P)
                    nc.tensor.matmul_mx(
                        out=acc[key][b],
                        lhsT=x_codes[:, x_cols].bitcast(FP8X4),
                        lhsT_scale=x_scales[:, x_cols],
                        rhs=w_codes[:, w_cols].bitcast(FP8X4),
                        rhs_scale=w_scales[:, w_cols],
                        start=(k_pass == 0),
                        stop=(k_pass == K // K_PASS - 1),
                    )


        def parent_term(acc, key):
            term = const.tile([P, B, W_GAUSS], F32, name="parent_" + key)
            for b in range(B):
                nc.vector.tensor_tensor(out=term[:, b], in0=acc[b], in1=bias[key], op=ALU.add)
            nc.vector.tensor_scalar(out=term, in0=term, scalar1=CLIP, scalar2=-CLIP, op0=ALU.min, op1=ALU.max)
            return term

        turned = {}

        def split_parents(key):
            def part(b, which):
                return parts[key, b][:, :, which, :].rearrange("p (g q) w -> p g q w", g=G)

            values = [parent[key][:, b].rearrange("p (q w g) -> p g q w", q=JGROUPS, g=G) for b in range(B)]
            for b in range(B):
                nc.vector.tensor_copy(out=part(b, 2), in_=values[b])
            for b in range(B):
                nc.vector.tensor_tensor(out=part(b, 3), in0=values[b], in1=part(b, 2), op=ALU.subtract)

        def turn_parts(key, b):
            if key not in turned:
                turned[key] = const.tile([P, GROUPS, B, P], BF16, name="turned_" + key)
            in_psum = psum_t.tile([P, GROUPS, P], BF16, name="turned_psum", tag="xt")
            for q in range(GROUPS):
                nc.tensor.transpose(
                    out=in_psum[:, q, :],
                    in_=parts[key, b][:, q].rearrange("p a w -> p (a w)"),
                    identity=ident_b,
                )
            turned_psum[key, b] = in_psum

        turned_psum = {}

        def take_parts(key, b, copy):
            copy(out=turned[key][:, :, b, :], in_=turned_psum[key, b])

        def pair_sums(key, ic, g, h):
            sums = psum_t.tile([P, 2, B * P], F32, name="sums", tag="xt")
            for l in range(2):
                nc.tensor.matmul(
                    out=sums[:, l, :],
                    lhsT=spread[key][:, ic * M : (ic + 1) * M],
                    rhs=turned[key][:, g * JGROUPS + 2 * h + l].rearrange("p b r -> p (b r)"),
                    start=True,
                    stop=True,
                )
            return sums

        logs, root, result = {}, {}, {}

        def log_of_sum(ic):
            logs[ic] = big.tile([P, G, JGROUPS, B * P], F32, name="logs", tag="big", align_bytes=64)
            for g in range(G):
                for h in range(2):
                    nc.scalar.activation(
                        out=logs[ic][:, g, 2 * h : 2 * h + 2, :], in_=pair_sums("var", ic, g, h), func=ACT.Ln
                    )

        def flat(tile4):
            return tile4.rearrange("p g q n -> p (g q n)")

        def inverse_root(ic):
            root[ic] = big.tile([P, G, JGROUPS, B * P], F32, name="root", tag="big", align_bytes=64)
            nc.scalar.activation(out=flat(root[ic]), in_=flat(logs[ic]), func=ACT.Exp, scale=-0.5)

        def weighed_difference(ic):
            for g in range(G):
                for h in range(2):
                    part = root[ic][:, g, 2 * h : 2 * h + 2, :]
                    nc.vector.tensor_tensor(out=part, in0=pair_sums("mean", ic, g, h), in1=part, op=ALU.mult)

        def square_difference(ic):
            nc.scalar.activation(out=flat(root[ic]), in_=flat(root[ic]), func=ACT.Square)

        def turn_back(ic, b):
            total = psum_acc.tile([P, NI, JGROUPS, M // NI], F32, name="total", tag="acc%d" % b)
            for q in range(JGROUPS):
                terms = [logs[ic][:, 0], logs[ic][:, 1], root[ic][:, 0], root[ic][:, 1]]
                for k, term in enumerate(terms):
                    nc.tensor.matmul(
                        out=total[:, :, q, :],
                        lhsT=term[:, q, b * P : (b + 1) * P],
                        rhs=ident_f,
                        start=(k == 0),
                        stop=(k == len(terms) - 1),
                        is_transpose=True,
                    )
            return total

        def add_child_term(ic, b):
            total = turn_back(ic, b)
            if b not in result:
                result[b] = big.tile([P, N_OUT], F32, name="result", tag="big", align_bytes=64)
            cols = slice(ic * (N_OUT // CHUNKS), (ic + 1) * (N_OUT // CHUNKS))
            nc.vector.scalar_tensor_tensor(
                out=result[b][:, cols],
                in0=total.rearrange("p i q m -> p (i q m)"),
                scalar=minus_half[:, b : b + 1],
                in1=child_term[b][:, cols],
                op0=ALU.mult,
                op1=ALU.add,
            )

        tw_terms = {}

        def transition_weights():
            tw = []
            for b in range(B):
                tw.append(const.tile([P, W_WEIGHT], F32, name="tw%d" % b))
                nc.vector.tensor_tensor(out=tw[b], in0=acc["weight"][b], in1=bias["weight"], op=ALU.add)
            for b in range(B):
                tw_terms[b] = const.tile([P, NL * NL, T, T], F32, name="tw_t%d" % b)
                nc.vector.tensor_scalar(
                    out=tw_terms[b],
                    in0=tw[b].rearrange("p (n u) -> p n u", u=T).unsqueeze(2).to_broadcast([P, NL * NL, T, T]),
                    scalar1=-LOG_2PI,
                    scalar2=both[:, b : b + 1],
                    op0=ALU.add,
                    op1=ALU.mult,
                )

        def add_transition_weight(ic, b):
            rows = result[b].rearrange("p (i m) -> p i m", i=NL)[:, ic * NI : (ic + 1) * NI]
            nc.vector.tensor_tensor(
                out=rows,
                in0=rows,
                in1=tw_terms[b].rearrange("p n t u -> p (n t u)").unsqueeze(1).to_broadcast([P, NI, NL * NL * T * T]),
                op=ALU.add,
            )
            store(ic, b)

        def store(ic, b):
            nc.sync.dma_start(
                out=out[b].rearrange("p i j k t e u -> p i (j k t e u)")[:, ic * NI : (ic + 1) * NI],
                in_=result[b].rearrange("p (i m) -> p i m", i=NL)[:, ic * NI : (ic + 1) * NI],
            )

        streams = (
            ("var", tpv_w, W_GAUSS, (3,)),
            ("mean", tpm_w, W_GAUSS, (2, 2, 4, 4, 4, 4, 4, 4)),
            ("weight", tw_w, W_WEIGHT, (2, 4, 4, 4)),
        )
        for key, w, width, vector_passes in streams:
            for s in range(K * width // (P * CHUNK)):
                pieces.append((key, w, width, vector_passes[s % len(vector_passes)], s))
        var_done = K * W_GAUSS // (P * CHUNK)
        mean_done = 2 * var_done
        last = len(pieces) - 1

        parent = {}

        def load(n):
            if n > last:
                return
            key, w, width, vector_passes, s = pieces[n]
            parts_of = LOAD_PARTS.get(n, 1)
            if n < X_CHUNKS:
                for part in range(parts_of):
                    load_x(n, part, parts_of)
            for part in range(parts_of):
                load_weights(n, w, width, s, part, parts_of)

        load(0)
        load_small()
        load_child()
        for n in range(1, AHEAD):
            load(n)
        def regroup(n):
            load(n + AHEAD)
            if n <= last:
                regroup_on_vector(n)
                regroup_on_scalar(n)

        for n in range(X_CHUNKS - 1):
            transpose_x(n)
            regroup(n)
            if n == 2:
                nc.scalar.activation(out=var1, in_=log_std1, func=ACT.Exp, scale=2.0)
            if n == 4:
                expand_child_weights(0, nc.scalar.copy)
            if n == 3:
                var_child_high_parts()
            if n == 4:
                var_child_low_parts()
            if n == 0:
                load_biases()
            if n == 4:
                turn_bias_rows()
            if n == 5:
                take_bias_cols()
            if n == 6:
                turn_bias_cols()
            quantise_x(n)
            quantise_weights(n)
            if n >= 1:
                multiply(n - 1)
            if n == 1:
                turn_masks()
                mean_child_parts()
                child_weights()
                mask_products()
                expand_child_weights(1, nc.vector.tensor_copy)
        n = X_CHUNKS - 1
        take_biases()
        transpose_x(n)
        regroup(n)
        quantise_x(n)
        multiply(n - 1)
        for part in range(2):
            quantise_weights(n, part, 2)
            multiply(n, part, 2)
        sv, ss, q, mx = regroup_on_vector, regroup_on_scalar, quantise_weights, multiply

        def prefetch(n):
            load(n + AHEAD)

        def first_half(key):
            parent[key] = parent_term(acc[key], key)
            if key == "var":
                nc.scalar.activation(out=parent[key], in_=parent[key], func=ACT.Exp, scale=2.0)

        def second_half(key):
            split_parents(key)
            for b in range(B):
                turn_parts(key, b)
            take_parts(key, 0, nc.scalar.copy)
            if key == "var":
                take_parts(key, 1, nc.scalar.copy)

        def differences(m):
            weighed_difference(m)
            square_difference(m)

        n = var_done
        prefetch(n)
        sv(n)
        ss(n)
        prefetch(n + 1)
        first_half("var")
        sv(n + 1)
        ss(n + 1)
        second_half("var")
        q(n)
        for r in range(CHUNKS):
            log_of_sum(r)
            if r == 0:
                mx(n)
            prefetch(n + 2 + r)
            sv(n + 2 + r)
            ss(n + 2 + r)
            q(n + 1 + r)
            mx(n + 1 + r)
        n = n + 6
        for r in range(2):
            prefetch(n + r)
            inverse_root(r)
            q(n - 1 + r)
            mx(n - 1 + r)
            sv(n + r)
            ss(n + 2 + r)
        n = n + 2
        for part in range(2):
            q(n - 1, part, 2)
            mx(n - 1, part, 2)
        sv(n)
        q(n)
        mx(n)
        first_half("mean")
        second_half("mean")
        sv(n + 1)
        take_parts("mean", 1, nc.vector.tensor_copy)
        ss(n + 2)
        inverse_root(2)
        q(n + 1)
        weighed_difference(0)
        square_difference(0)
        weighed_difference(1)
        square_difference(1)
        mx(n + 1)
        inverse_root(3)
        sv(n + 2)
        weighed_difference(2)
        square_difference(2)
        q(n + 2)
        for b in range(B):
            add_child_term(0, b)
        ss(n + 3)
        sv(n + 3)
        mx(n + 2)
        weighed_difference(3)
        square_difference(3)
        q(n + 3)
        for b in range(B):
            add_child_term(1, b)
        mx(n + 3)
        transition_weights()
        for b in range(B):
            rows = child_term[b].rearrange("p (i m) -> p i m", i=NL)[:, NL - 2 * NI :]
            nc.vector.tensor_tensor(
                out=rows,
                in0=rows,
                in1=tw_terms[b].rearrange("p n t u -> p (n t u)").unsqueeze(1).to_broadcast([P, 2 * NI, NL * NL * T * T]),
                op=ALU.add,
            )
        for ic in range(CHUNKS - 2):
            for b in range(B):
                add_transition_weight(ic, b)
        for ic in range(CHUNKS - 2, CHUNKS):
            for b in range(B):
                add_child_term(ic, b)
                store(ic, b)
